import numpy as np
import ml_dtypes


def mxq(x, axis, fmt="e4m3"):
    dtype, down = {"e4m3": (ml_dtypes.float8_e4m3fn, 7), "e5m2": (ml_dtypes.float8_e5m2, 14)}[fmt]
    v = np.moveaxis(np.asarray(x, np.float32).astype(ml_dtypes.bfloat16).astype(np.float64), axis, -1)
    blocks = v.reshape(v.shape[:-1] + (-1, 32))
    amax = np.abs(blocks).max(-1, keepdims=True)
    byte = np.maximum(np.where(amax > 0, np.frexp(amax)[1] - 1 + 127, 0) - down, 1)
    scale = np.exp2(byte - 127.0)
    codes = (blocks / scale).astype(np.float32).astype(dtype).astype(np.float64)
    return np.moveaxis((codes * scale).reshape(v.shape), -1, axis)


WIDE = False


def mx_kscale(k):
    if not WIDE:
        return np.ones(k)
    levels = np.array([10, -10, 5, -5, 0])
    a = np.random.permutation(np.resize(levels, k // 512 * 4)).reshape(k // 512, 4)
    idx = np.arange(k)
    return np.exp2(a[idx // 512, idx % 128 // 32])


BF16 = ml_dtypes.bfloat16


def bf(x):
    return np.asarray(x, np.float32).astype(BF16)


def f64(x):
    return np.asarray(x).astype(np.float64)


E2M1 = np.array([0.0, 0.5, 1.0, 1.5, 2.0, 3.0, 4.0, 6.0, -0.0, -0.5, -1.0, -1.5, -2.0, -3.0, -4.0, -6.0])


def pack_weight(w, fmt):
    k, n = w.shape
    w = f64(bf(w)).reshape(k // 32, 32, n)
    amax = np.abs(w).max(1)
    if fmt == "e4m3":
        byte = np.frexp(amax)[1] - 1 + 127 - 7
    else:
        mant, ex = np.frexp(amax / 6.0)
        byte = np.where(mant > 0.5, ex, ex - 1) + 127
    byte = np.clip(np.where(amax > 0, byte, 1), 1, 254)
    scaled = (w * np.exp2(127.0 - byte)[:, None, :]).reshape(k, n).astype(np.float32)
    by_word = np.ascontiguousarray(scaled.reshape(k // 512, 128, 4, n).transpose(0, 1, 3, 2))
    if fmt == "e4m3":
        words = by_word.astype(ml_dtypes.float8_e4m3fn).view(np.uint8)
    else:
        c = by_word.astype(ml_dtypes.float4_e2m1fn).view(np.uint8) & 0xF
        words = c[..., 0::2] | (c[..., 1::2] << 4)
    return np.ascontiguousarray(words), np.ascontiguousarray(byte.astype(np.uint8).reshape(k // 512, 16, n))


def unpack_weight(words, scales, fmt):
    g, p, n, _ = words.shape
    if fmt == "e4m3":
        vals = np.ascontiguousarray(words).view(ml_dtypes.float8_e4m3fn).astype(np.float64)
    else:
        nib = np.empty((g, p, n, 4), np.uint8)
        nib[..., 0::2] = words & 0xF
        nib[..., 1::2] = words >> 4
        vals = E2M1[nib]
    vals = vals * np.repeat(np.exp2(scales.astype(np.float64) - 127.0), 8, axis=1)[..., None]
    return vals.transpose(0, 1, 3, 2).reshape(g * 512, n)


E, B, IN, H, O = 5, 896, 71, 1024, 64
O2 = O + O
FMT = "e4m3"


def silu(v):
    return v / (1.0 + np.exp(-v))


def softplus(v):
    return np.maximum(v, 0.0) + np.log(1.0 + np.exp(-np.abs(v)))


def setup_inputs():
    s = mx_kscale(H)
    h2 = bf(silu(np.random.standard_normal((E, B, H))) * s)
    w3 = np.random.standard_normal((E, H, H)) * 1.6 / np.sqrt(H) / s[:, None]
    w3_words, w3_scales = pack_weight(w3.reshape(-1, H), FMT)
    b3 = bf(np.random.standard_normal((E, 1, H)) * 0.2)
    w4 = np.random.standard_normal((E, H, O2)) * 2.5 / np.sqrt(H)
    w4_words, w4_scales = pack_weight(w4.reshape(-1, O2), FMT)
    b4 = bf(np.random.standard_normal((E, 1, O2)) * 0.2)
    max_logvar = bf(0.5 + 0.1 * np.random.standard_normal((1, O)))
    min_logvar = bf(-1.5 + 0.1 * np.random.standard_normal((1, O)))
    return {"h2": h2,
            "w3_words": w3_words,
            "w3_scales": w3_scales,
            "b3": b3,
            "w4_words": w4_words,
            "w4_scales": w4_scales,
            "b4": b4,
            "max_logvar": max_logvar,
            "min_logvar": min_logvar}


def reference(h2, w3_words, w3_scales, b3, w4_words, w4_scales, b4, max_logvar, min_logvar):
    h3 = silu((mxq(f64(h2), 2, "e4m3") @ unpack_weight(w3_words, w3_scales, FMT).reshape(E, H, H)) + f64(b3))
    o = (mxq(h3, 2, "e4m3") @ unpack_weight(w4_words, w4_scales, FMT).reshape(E, H, O2)) + f64(b4)
    mean, logvar = o[..., :O], o[..., O:]
    logvar = f64(max_logvar) - softplus(f64(max_logvar) - logvar)
    logvar = f64(min_logvar) + softplus(logvar - f64(min_logvar))
    return mean, logvar

@@ -1,0 +1,340 @@
+from contextlib import ExitStack
+
+import concourse.mybir as mybir
+from concourse.masks import make_identity
+
+F32 = mybir.dt.float32
+BF16 = mybir.dt.bfloat16
+I32 = mybir.dt.int32
+U32 = mybir.dt.uint32
+U8 = mybir.dt.uint8
+FP8X4 = mybir.dt.float8_e4m3fn_x4
+ACT = mybir.ActivationFunctionType
+ALU = mybir.AluOpType
+
+MEMBERS = 5
+BATCH = 896
+HIDDEN = 1024
+OUT = 64
+OUT2 = 2 * OUT
+
+P = 128
+PACK = 4
+K_PASS = P * PACK
+PASSES = HIDDEN // K_PASS
+BANK = 512
+HALVES = HIDDEN // BANK
+UNITS_PER_MEMBER = BATCH // P
+UNITS = MEMBERS * UNITS_PER_MEMBER
+WORDS = HIDDEN // 2
+PLANES_PER_TILE = 4
+GROUP = BANK // OUT2
+
+LEAD_A = 1
+LAG_SILU = 1
+LAG_C = 3
+LAG_D = 4
+
+FLOPS = 2 * MEMBERS * BATCH * HIDDEN * (HIDDEN + OUT2)
+
+
+def tile_ensembledynamicsmodel_pa_t_e_kernel(
+    tc, h2, w3_words, w3_scales, b3, w4_words, w4_scales, b4, max_logvar, min_logvar, out_0, out_1
+):
+    nc = tc.nc
+    with ExitStack() as ctx:
+        keep = ctx.enter_context(tc.tile_pool(name="keep", bufs=1))
+        member_pool = ctx.enter_context(tc.tile_pool(name="member", bufs=3))
+        work = ctx.enter_context(tc.tile_pool(name="work", bufs=3))
+        tail = ctx.enter_context(tc.tile_pool(name="tail", bufs=2))
+        psum = ctx.enter_context(tc.psum_pool(name="psum", bufs=1))
+        ctx.enter_context(tc.manual_schedule())
+
+        ident = keep.tile([P, P], F32)
+        make_identity(nc, ident[:])
+        half = keep.tile([P, 1], F32)
+        nc.vector.memset(half[:], 0.5)
+        warm = keep.tile([P, 1], F32)
+        nc.scalar.activation(out=warm[:], in_=half[:], func=ACT.Silu)
+
+        n_plane_tiles = (MEMBERS * PASSES + PLANES_PER_TILE - 1) // PLANES_PER_TILE
+        w3_planes = keep.tile([P, n_plane_tiles, HIDDEN], U8, align_bytes=64)
+        nc.vector.memset(w3_planes[:].rearrange("p a n -> p (a n)").bitcast(I32), 0)
+        w4_planes = keep.tile([P, MEMBERS * PASSES, OUT2], U8, align_bytes=64)
+        nc.vector.memset(w4_planes[:].rearrange("p c n -> p (c n)").bitcast(I32), 0)
+        w4_codes = keep.tile([P, MEMBERS * PASSES, OUT2], U32, align_bytes=64)
+
+        b4_all = keep.tile([P, MEMBERS, OUT2], BF16)
+        max_lv = keep.tile([P, OUT], BF16)
+        min_lv = keep.tile([P, OUT], BF16)
+        shift = keep.tile([P, MEMBERS, OUT2], F32)
+        span = keep.tile([P, OUT], F32)
+        results = keep.tile([P, 2, UNITS, OUT], F32)
+
+        h2_of = {}
+        w3_of = {}
+        b3_of = {}
+
+        def load_h2_unit(e, j):
+            rows = h2[e].rearrange("(p j) k -> p j k", j=UNITS_PER_MEMBER)
+            nc.sync.dma_start(out=h2_of[e][:, j, :], in_=rows[:, j, :])
+
+        def load_w3_planes(a):
+            first = a * PLANES_PER_TILE
+            n_planes = min(PLANES_PER_TILE, MEMBERS * PASSES - first)
+            for quadrant in range(4):
+                nc.sync.dma_start(
+                    out=w3_planes[32 * quadrant : 32 * quadrant + 4 * n_planes, a, :].bitcast(I32),
+                    in_=w3_scales[first : first + n_planes, 4 * quadrant : 4 * quadrant + 4, :].bitcast(I32),
+                )
+
+        def load_w3_codes(e):
+            for half_n in range(HALVES):
+                for g in range(PASSES):
+                    words = w3_words[PASSES * e + g].rearrange("p n t -> p (n t)")
+                    nc.sync.dma_start(
+                        out=w3_of[e][:, g, half_n * BANK : (half_n + 1) * BANK].bitcast(I32),
+                        in_=words[:, half_n * BANK * PACK : (half_n + 1) * BANK * PACK].bitcast(I32),
+                    )
+
+        def new_member_tiles(e):
+            h2_of[e] = member_pool.tile([P, UNITS_PER_MEMBER, HIDDEN], BF16, name="h2_%d" % e, tag="h2")
+            w3_of[e] = member_pool.tile([P, PASSES, HIDDEN], U32, name="w3_%d" % e, tag="w3", align_bytes=64)
+            b3_of[e] = member_pool.tile([P, HIDDEN], BF16, name="b3_%d" % e, tag="b3")
+
+        def load_member(e):
+            new_member_tiles(e)
+            load_w3_codes(e)
+            nc.sync.dma_start(out=b3_of[e][:], in_=b3[e, 0, :].partition_broadcast(P))
+            for j in range(UNITS_PER_MEMBER):
+                load_h2_unit(e, j)
+
+        new_member_tiles(0)
+        load_h2_unit(0, 0)
+        load_w3_planes(0)
+        load_w3_codes(0)
+        nc.sync.dma_start(out=b3_of[0][:], in_=b3[0, 0, :].partition_broadcast(P))
+        for j in range(1, UNITS_PER_MEMBER):
+            load_h2_unit(0, j)
+        for quadrant in range(4):
+            nc.sync.dma_start(
+                out=w4_planes[32 * quadrant : 32 * quadrant + 4, :, :].bitcast(I32),
+                in_=w4_scales[:, 4 * quadrant : 4 * quadrant + 4, :].rearrange("c r n -> r c n").bitcast(I32),
+            )
+        nc.sync.dma_start(
+            out=w4_codes[:].bitcast(I32),
+            in_=w4_words.rearrange("c p n t -> p c (n t)").bitcast(I32),
+        )
+        nc.sync.dma_start(
+            out=b4_all[:].rearrange("p e n -> p (e n)"),
+            in_=b4.rearrange("e o n -> (e o n)").partition_broadcast(P),
+        )
+        nc.sync.dma_start(out=max_lv[:], in_=max_logvar[0, :].partition_broadcast(P))
+        nc.sync.dma_start(out=min_lv[:], in_=min_logvar[0, :].partition_broadcast(P))
+        for a in range(1, n_plane_tiles):
+            load_w3_planes(a)
+        load_member(1)
+
+        nc.vector.tensor_copy(out=shift[:, :, 0:OUT], in_=b4_all[:, :, 0:OUT])
+        nc.vector.tensor_tensor(
+            out=shift[:, :, OUT:OUT2],
+            in0=b4_all[:, :, OUT:OUT2],
+            in1=max_lv[:].unsqueeze(1).to_broadcast([P, MEMBERS, OUT]),
+            op=ALU.subtract,
+        )
+        nc.vector.tensor_tensor(out=span[:], in0=max_lv[:], in1=min_lv[:], op=ALU.subtract)
+
+        turned_of = {}
+        codes_of = {}
+        sums_of = {}
+        z_of = {}
+        h3_of = {}
+        head_of = {}
+
+        def transpose_words(stage, i, words, step):
+            bank = psum.tile([P, PASSES * 2, P], F32, name="turned_%s_%d" % (stage, i), tag="turned_" + stage)
+            for g in range(PASSES):
+                for u in range(2):
+                    if step == 2:
+                        block = words[:, 256 * g + u : 256 * (g + 1) : 2]
+                    else:
+                        block = words[:, (2 * g + u) * P : (2 * g + u + 1) * P]
+                    nc.tensor.transpose(out=bank[:, 2 * g + u, :], in_=block, identity=ident[:])
+            turned_of[(stage, i)] = bank
+
+        def copy_out(stage, i):
+            grouped = work.tile([P, HIDDEN], BF16, name="grouped_%s_%d" % (stage, i), tag="grouped_" + stage, align_bytes=64)
+            nc.scalar.copy(
+                out=grouped[:].bitcast(F32).rearrange("p (g r u) -> p g r u", g=PASSES, u=2),
+                in_=turned_of[(stage, i)][:].rearrange("p (g u) r -> p g r u", u=2),
+            )
+            return grouped
+
+        def quantise(stage, i, grouped):
+            codes = work.tile([P, PASSES * P], U32, name="codes_%s_%d" % (stage, i), tag="codes_" + stage, align_bytes=64)
+            plane = work.tile([P, PASSES * P], U8, name="plane_%s_%d" % (stage, i), tag="plane_" + stage, align_bytes=64)
+            nc.vector.quantize_mx(out=codes[:].bitcast(FP8X4), scales=plane[:], in_=grouped[:])
+            codes_of[(stage, i)] = (codes, plane)
+
+        def first_matmul(i):
+            e = i // UNITS_PER_MEMBER
+            codes, plane = codes_of[("a", i)]
+            for half_n in range(HALVES):
+                cols = slice(half_n * BANK, (half_n + 1) * BANK)
+                sums = psum.tile([P, BANK], F32, name="sums_%d_%d" % (i, half_n), tag="sums", bufs=4)
+                for g in range(PASSES):
+                    c = PASSES * e + g
+                    rows = slice(g * P, (g + 1) * P)
+                    nc.tensor.matmul_mx(
+                        out=sums[:],
+                        lhsT=codes[:, rows].bitcast(FP8X4),
+                        lhsT_scale=plane[:, rows],
+                        rhs=w3_of[e][:, g, cols].bitcast(FP8X4),
+                        rhs_scale=w3_planes[4 * (c % PLANES_PER_TILE) : P, c // PLANES_PER_TILE, cols],
+                        start=(g == 0),
+                        stop=(g == PASSES - 1),
+                    )
+                sums_of[(i, half_n)] = sums
+
+        def add_b3(i):
+            e = i // UNITS_PER_MEMBER
+            z = work.tile([P, HIDDEN], F32, name="z_%d" % i, tag="z")
+            for half_n in range(HALVES):
+                cols = slice(half_n * BANK, (half_n + 1) * BANK)
+                nc.vector.tensor_tensor(
+                    out=z[:, cols].rearrange("p (u q e) -> p u q e", u=2, e=2),
+                    in0=sums_of[(i, half_n)][:].rearrange("p (q u e) -> p u q e", u=2, e=2),
+                    in1=b3_of[e][:, cols].rearrange("p (q u e) -> p u q e", u=2, e=2),
+                    op=ALU.add,
+                )
+            z_of[i] = z
+
+        def silu(i):
+            h3 = work.tile([P, HIDDEN], BF16, name="h3_%d" % i, tag="h3", bufs=4)
+            nc.scalar.activation(out=h3[:], in_=z_of[i][:], func=ACT.Silu)
+            h3_of[i] = h3
+
+        def second_matmul(i):
+            e = i // UNITS_PER_MEMBER
+            slot = (i % UNITS_PER_MEMBER) % GROUP
+            if slot == 0:
+                head_of[e] = psum.tile([P, GROUP, OUT2], F32, name="head_%d" % i, tag="head", bufs=2)
+            codes, plane = codes_of[("c", i)]
+            for g in range(PASSES):
+                rows = slice(g * P, (g + 1) * P)
+                nc.tensor.matmul_mx(
+                    out=head_of[e][:, slot, :],
+                    lhsT=codes[:, rows].bitcast(FP8X4),
+                    lhsT_scale=plane[:, rows],
+                    rhs=w4_codes[:, PASSES * e + g, :].bitcast(FP8X4),
+                    rhs_scale=w4_planes[:, PASSES * e + g, :],
+                    start=(g == 0),
+                    stop=(g == PASSES - 1),
+                )
+
+        def add_b4(i):
+            e = i // UNITS_PER_MEMBER
+            n = (i % UNITS_PER_MEMBER) % GROUP + 1
+            nc.vector.tensor_tensor(
+                out=results[:, :, i + 1 - n : i + 1, :].rearrange("p h j o -> p j h o"),
+                in0=head_of[e][:, 0:n, :].rearrange("p j (h o) -> p j h o", h=2),
+                in1=shift[:, e, :].rearrange("p (h o) -> p h o", h=2).unsqueeze(1).to_broadcast([P, n, 2, OUT]),
+                op=ALU.add,
+            )
+
+        clipped_of = {}
+        tanh_of = {}
+
+        def begin_bounds(e):
+            units = slice(e * UNITS_PER_MEMBER, (e + 1) * UNITS_PER_MEMBER)
+            nc.sync.dma_start(
+                out=out_0[e].rearrange("(p j) o -> p (j o)", j=UNITS_PER_MEMBER),
+                in_=results[:, 0, units, :].rearrange("p j o -> p (j o)"),
+            )
+            u = results[:, 1, units, :]
+            size = tail.tile([P, UNITS_PER_MEMBER, OUT], F32, name="size_%d" % e, tag="size")
+            nc.vector.scalar_tensor_tensor(out=size[:], in0=u, scalar=-1.0, in1=u, op0=ALU.mult, op1=ALU.max)
+            clipped = tail.tile([P, UNITS_PER_MEMBER, OUT], F32, name="clipped_%d" % e, tag="clipped", bufs=MEMBERS)
+            nc.vector.scalar_tensor_tensor(
+                out=clipped[:],
+                in0=u,
+                scalar=0.0,
+                in1=span[:].unsqueeze(1).to_broadcast([P, UNITS_PER_MEMBER, OUT]),
+                op0=ALU.min,
+                op1=ALU.add,
+            )
+            tanh = tail.tile([P, UNITS_PER_MEMBER, OUT], F32, name="tanh_%d" % e, tag="tanh", bufs=MEMBERS)
+            nc.scalar.activation(out=tanh[:], in_=size[:], func=ACT.Tanh, scale=0.5)
+            clipped_of[e] = clipped
+            tanh_of[e] = tanh
+
+        for r in range(-LEAD_A, UNITS + LAG_D):
+            unit_a = r + LEAD_A
+            unit_c = r - LAG_C
+            unit_d = r - LAG_D
+            unit_s = r - LAG_SILU
+            if 0 <= r < UNITS and r % UNITS_PER_MEMBER == 0 and r // UNITS_PER_MEMBER + 2 < MEMBERS:
+                load_member(r // UNITS_PER_MEMBER + 2)
+
+            if 0 <= unit_c < UNITS:
+                transpose_words("c", unit_c, h3_of[unit_c][:].bitcast(F32), 1)
+            if unit_a < UNITS:
+                e_a = unit_a // UNITS_PER_MEMBER
+                transpose_words("a", unit_a, h2_of[e_a][:, unit_a % UNITS_PER_MEMBER, :].bitcast(F32), 2)
+            if 0 <= unit_d < UNITS:
+                second_matmul(unit_d)
+            if 0 <= r < UNITS:
+                first_matmul(r)
+
+            grouped_c = copy_out("c", unit_c) if 0 <= unit_c < UNITS else None
+            grouped_a = copy_out("a", unit_a) if unit_a < UNITS else None
+            if 0 <= unit_s < UNITS:
+                silu(unit_s)
+
+            if grouped_c is not None:
+                quantise("c", unit_c, grouped_c)
+            if grouped_a is not None:
+                quantise("a", unit_a, grouped_a)
+            if 0 <= unit_d < UNITS:
+                place = unit_d % UNITS_PER_MEMBER
+                if place % GROUP == GROUP - 1 or place == UNITS_PER_MEMBER - 1:
+                    add_b4(unit_d)
+                if place == UNITS_PER_MEMBER - 1:
+                    begin_bounds(unit_d // UNITS_PER_MEMBER)
+            if 0 <= r < UNITS:
+                add_b3(r)
+
+        shape = [P, UNITS_PER_MEMBER, OUT]
+        size2_of = {}
+        floor_of = {}
+        for e in range(MEMBERS):
+            log1 = tail.tile(shape, F32, name="log1_%d" % e, tag="log1")
+            nc.scalar.activation(out=log1[:], in_=tanh_of[e][:], func=ACT.Ln, scale=0.5, bias=half[:])
+            v = tail.tile(shape, F32, name="v_%d" % e, tag="v")
+            nc.vector.tensor_tensor(out=v[:], in0=clipped_of[e][:], in1=log1[:], op=ALU.add)
+            size2_of[e] = tail.tile(shape, F32, name="size2_%d" % e, tag="size2", bufs=MEMBERS)
+            nc.vector.scalar_tensor_tensor(
+                out=size2_of[e][:], in0=v[:], scalar=-1.0, in1=v[:], op0=ALU.mult, op1=ALU.max
+            )
+            floor_of[e] = tail.tile(shape, F32, name="floor_%d" % e, tag="floor", bufs=MEMBERS)
+            nc.vector.scalar_tensor_tensor(
+                out=floor_of[e][:],
+                in0=v[:],
+                scalar=0.0,
+                in1=min_lv[:].unsqueeze(1).to_broadcast(shape),
+                op0=ALU.max,
+                op1=ALU.add,
+            )
+        tanh2_of = {}
+        for e in range(MEMBERS):
+            tanh2_of[e] = tail.tile(shape, F32, name="tanh2_%d" % e, tag="tanh2", bufs=MEMBERS)
+            nc.scalar.activation(out=tanh2_of[e][:], in_=size2_of[e][:], func=ACT.Tanh, scale=0.5)
+        for e in range(MEMBERS):
+            log2 = tail.tile(shape, F32, name="log2_%d" % e, tag="log2")
+            nc.scalar.activation(out=log2[:], in_=tanh2_of[e][:], func=ACT.Ln, scale=0.5, bias=half[:])
+            logvar = tail.tile(shape, F32, name="logvar_%d" % e, tag="logvar")
+            nc.vector.tensor_tensor(out=logvar[:], in0=floor_of[e][:], in1=log2[:], op=ALU.subtract)
+            nc.sync.dma_start(
+                out=out_1[e].rearrange("(p j) o -> p (j o)", j=UNITS_PER_MEMBER),
+                in_=logvar[:].rearrange("p j o -> p (j o)"),
+            )

@@ -23,17 +23,12 @@ PACK = 4
 K_PASS = P * PACK
 PASSES = HIDDEN // K_PASS
 BANK = 512
-HALVES = HIDDEN // BANK
-UNITS_PER_MEMBER = BATCH // P
-UNITS = MEMBERS * UNITS_PER_MEMBER
-WORDS = HIDDEN // 2
+UNITS = BATCH // P
+CHUNKS = ((0, 512), (512, 768), (768, 896))
 PLANES_PER_TILE = 4
-GROUP = BANK // OUT2
-
-LEAD_A = 1
-LAG_SILU = 1
-LAG_C = 3
-LAG_D = 4
+HEAD_GROUPS = ((0, 4), (4, 7))
+STEPS = 4
+UNITS_PER_STEP = 2
 
 FLOPS = 2 * MEMBERS * BATCH * HIDDEN * (HIDDEN + OUT2)
 
@@ -42,13 +37,11 @@ def tile_ensembledynamicsmodel_pa_t_e_kernel(
     tc, h2, w3_words, w3_scales, b3, w4_words, w4_scales, b4, max_logvar, min_logvar, out_0, out_1
 ):
     nc = tc.nc
-    with ExitStack() as ctx:
-        keep = ctx.enter_context(tc.tile_pool(name="keep", bufs=1))
-        member_pool = ctx.enter_context(tc.tile_pool(name="member", bufs=3))
-        work = ctx.enter_context(tc.tile_pool(name="work", bufs=3))
-        tail = ctx.enter_context(tc.tile_pool(name="tail", bufs=2))
-        psum = ctx.enter_context(tc.psum_pool(name="psum", bufs=1))
-        ctx.enter_context(tc.manual_schedule())
+    member_shape = [P, UNITS, OUT]
+    with ExitStack() as whole:
+        keep = whole.enter_context(tc.tile_pool(name="keep", bufs=1))
+        bounds = whole.enter_context(tc.tile_pool(name="bounds", bufs=MEMBERS))
+        whole.enter_context(tc.manual_schedule())
 
         ident = keep.tile([P, P], F32)
         make_identity(nc, ident[:])
@@ -57,284 +50,353 @@ def tile_ensembledynamicsmodel_pa_t_e_kernel(
         warm = keep.tile([P, 1], F32)
         nc.scalar.activation(out=warm[:], in_=half[:], func=ACT.Silu)
 
-        n_plane_tiles = (MEMBERS * PASSES + PLANES_PER_TILE - 1) // PLANES_PER_TILE
+        n_passes = MEMBERS * PASSES
+        n_plane_tiles = (n_passes + PLANES_PER_TILE - 1) // PLANES_PER_TILE
+        w3_planes_raw = keep.tile([P, n_plane_tiles, HIDDEN], U8)
+        nc.vector.memset(w3_planes_raw[:].rearrange("p a n -> p (a n)").bitcast(I32), 0)
         w3_planes = keep.tile([P, n_plane_tiles, HIDDEN], U8, align_bytes=64)
-        nc.vector.memset(w3_planes[:].rearrange("p a n -> p (a n)").bitcast(I32), 0)
-        w4_planes = keep.tile([P, MEMBERS * PASSES, OUT2], U8, align_bytes=64)
+        w4_planes = keep.tile([P, n_passes, OUT2], U8, align_bytes=64)
         nc.vector.memset(w4_planes[:].rearrange("p c n -> p (c n)").bitcast(I32), 0)
-        w4_codes = keep.tile([P, MEMBERS * PASSES, OUT2], U32, align_bytes=64)
+        w4_codes = keep.tile([P, n_passes, OUT2], U32, align_bytes=64)
 
+        b3_rows = keep.tile([P, P], BF16)
+        nc.vector.memset(b3_rows[:], 0.0)
+        b3_rows_f32 = keep.tile([P, P], F32)
+        b3_columns = keep.tile([P, MEMBERS * PASSES * STEPS], F32)
         b4_all = keep.tile([P, MEMBERS, OUT2], BF16)
         max_lv = keep.tile([P, OUT], BF16)
         min_lv = keep.tile([P, OUT], BF16)
         shift = keep.tile([P, MEMBERS, OUT2], F32)
         span = keep.tile([P, OUT], F32)
-        results = keep.tile([P, 2, UNITS, OUT], F32)
-
-        h2_of = {}
-        w3_of = {}
-        b3_of = {}
-
-        def load_h2_unit(e, j):
-            rows = h2[e].rearrange("(p j) k -> p j k", j=UNITS_PER_MEMBER)
-            nc.sync.dma_start(out=h2_of[e][:, j, :], in_=rows[:, j, :])
-
-        def load_w3_planes(a):
-            first = a * PLANES_PER_TILE
-            n_planes = min(PLANES_PER_TILE, MEMBERS * PASSES - first)
-            for quadrant in range(4):
-                nc.sync.dma_start(
-                    out=w3_planes[32 * quadrant : 32 * quadrant + 4 * n_planes, a, :].bitcast(I32),
-                    in_=w3_scales[first : first + n_planes, 4 * quadrant : 4 * quadrant + 4, :].bitcast(I32),
-                )
-
-        def load_w3_codes(e):
-            for half_n in range(HALVES):
-                for g in range(PASSES):
-                    words = w3_words[PASSES * e + g].rearrange("p n t -> p (n t)")
-                    nc.sync.dma_start(
-                        out=w3_of[e][:, g, half_n * BANK : (half_n + 1) * BANK].bitcast(I32),
-                        in_=words[:, half_n * BANK * PACK : (half_n + 1) * BANK * PACK].bitcast(I32),
-                    )
-
-        def new_member_tiles(e):
-            h2_of[e] = member_pool.tile([P, UNITS_PER_MEMBER, HIDDEN], BF16, name="h2_%d" % e, tag="h2")
-            w3_of[e] = member_pool.tile([P, PASSES, HIDDEN], U32, name="w3_%d" % e, tag="w3", align_bytes=64)
-            b3_of[e] = member_pool.tile([P, HIDDEN], BF16, name="b3_%d" % e, tag="b3")
-
-        def load_member(e):
-            new_member_tiles(e)
-            load_w3_codes(e)
-            nc.sync.dma_start(out=b3_of[e][:], in_=b3[e, 0, :].partition_broadcast(P))
-            for j in range(UNITS_PER_MEMBER):
-                load_h2_unit(e, j)
-
-        new_member_tiles(0)
-        load_h2_unit(0, 0)
-        load_w3_planes(0)
-        load_w3_codes(0)
-        nc.sync.dma_start(out=b3_of[0][:], in_=b3[0, 0, :].partition_broadcast(P))
-        for j in range(1, UNITS_PER_MEMBER):
-            load_h2_unit(0, j)
-        for quadrant in range(4):
-            nc.sync.dma_start(
-                out=w4_planes[32 * quadrant : 32 * quadrant + 4, :, :].bitcast(I32),
-                in_=w4_scales[:, 4 * quadrant : 4 * quadrant + 4, :].rearrange("c r n -> r c n").bitcast(I32),
-            )
-        nc.sync.dma_start(
-            out=w4_codes[:].bitcast(I32),
-            in_=w4_words.rearrange("c p n t -> p c (n t)").bitcast(I32),
-        )
-        nc.sync.dma_start(
-            out=b4_all[:].rearrange("p e n -> p (e n)"),
-            in_=b4.rearrange("e o n -> (e o n)").partition_broadcast(P),
-        )
-        nc.sync.dma_start(out=max_lv[:], in_=max_logvar[0, :].partition_broadcast(P))
-        nc.sync.dma_start(out=min_lv[:], in_=min_logvar[0, :].partition_broadcast(P))
-        for a in range(1, n_plane_tiles):
-            load_w3_planes(a)
-        load_member(1)
-
-        nc.vector.tensor_copy(out=shift[:, :, 0:OUT], in_=b4_all[:, :, 0:OUT])
-        nc.vector.tensor_tensor(
-            out=shift[:, :, OUT:OUT2],
-            in0=b4_all[:, :, OUT:OUT2],
-            in1=max_lv[:].unsqueeze(1).to_broadcast([P, MEMBERS, OUT]),
-            op=ALU.subtract,
-        )
-        nc.vector.tensor_tensor(out=span[:], in0=max_lv[:], in1=min_lv[:], op=ALU.subtract)
-
-        turned_of = {}
-        codes_of = {}
-        sums_of = {}
-        z_of = {}
-        h3_of = {}
-        head_of = {}
-
-        def transpose_words(stage, i, words, step):
-            bank = psum.tile([P, PASSES * 2, P], F32, name="turned_%s_%d" % (stage, i), tag="turned_" + stage)
-            for g in range(PASSES):
-                for u in range(2):
-                    if step == 2:
-                        block = words[:, 256 * g + u : 256 * (g + 1) : 2]
-                    else:
-                        block = words[:, (2 * g + u) * P : (2 * g + u + 1) * P]
-                    nc.tensor.transpose(out=bank[:, 2 * g + u, :], in_=block, identity=ident[:])
-            turned_of[(stage, i)] = bank
-
-        def copy_out(stage, i):
-            grouped = work.tile([P, HIDDEN], BF16, name="grouped_%s_%d" % (stage, i), tag="grouped_" + stage, align_bytes=64)
-            nc.scalar.copy(
-                out=grouped[:].bitcast(F32).rearrange("p (g r u) -> p g r u", g=PASSES, u=2),
-                in_=turned_of[(stage, i)][:].rearrange("p (g u) r -> p g r u", u=2),
-            )
-            return grouped
-
-        def quantise(stage, i, grouped):
-            codes = work.tile([P, PASSES * P], U32, name="codes_%s_%d" % (stage, i), tag="codes_" + stage, align_bytes=64)
-            plane = work.tile([P, PASSES * P], U8, name="plane_%s_%d" % (stage, i), tag="plane_" + stage, align_bytes=64)
-            nc.vector.quantize_mx(out=codes[:].bitcast(FP8X4), scales=plane[:], in_=grouped[:])
-            codes_of[(stage, i)] = (codes, plane)
-
-        def first_matmul(i):
-            e = i // UNITS_PER_MEMBER
-            codes, plane = codes_of[("a", i)]
-            for half_n in range(HALVES):
-                cols = slice(half_n * BANK, (half_n + 1) * BANK)
-                sums = psum.tile([P, BANK], F32, name="sums_%d_%d" % (i, half_n), tag="sums", bufs=4)
-                for g in range(PASSES):
-                    c = PASSES * e + g
-                    rows = slice(g * P, (g + 1) * P)
-                    nc.tensor.matmul_mx(
-                        out=sums[:],
-                        lhsT=codes[:, rows].bitcast(FP8X4),
-                        lhsT_scale=plane[:, rows],
-                        rhs=w3_of[e][:, g, cols].bitcast(FP8X4),
-                        rhs_scale=w3_planes[4 * (c % PLANES_PER_TILE) : P, c // PLANES_PER_TILE, cols],
-                        start=(g == 0),
-                        stop=(g == PASSES - 1),
-                    )
-                sums_of[(i, half_n)] = sums
-
-        def add_b3(i):
-            e = i // UNITS_PER_MEMBER
-            z = work.tile([P, HIDDEN], F32, name="z_%d" % i, tag="z")
-            for half_n in range(HALVES):
-                cols = slice(half_n * BANK, (half_n + 1) * BANK)
-                nc.vector.tensor_tensor(
-                    out=z[:, cols].rearrange("p (u q e) -> p u q e", u=2, e=2),
-                    in0=sums_of[(i, half_n)][:].rearrange("p (q u e) -> p u q e", u=2, e=2),
-                    in1=b3_of[e][:, cols].rearrange("p (q u e) -> p u q e", u=2, e=2),
-                    op=ALU.add,
-                )
-            z_of[i] = z
-
-        def silu(i):
-            h3 = work.tile([P, HIDDEN], BF16, name="h3_%d" % i, tag="h3", bufs=4)
-            nc.scalar.activation(out=h3[:], in_=z_of[i][:], func=ACT.Silu)
-            h3_of[i] = h3
-
-        def second_matmul(i):
-            e = i // UNITS_PER_MEMBER
-            slot = (i % UNITS_PER_MEMBER) % GROUP
-            if slot == 0:
-                head_of[e] = psum.tile([P, GROUP, OUT2], F32, name="head_%d" % i, tag="head", bufs=2)
-            codes, plane = codes_of[("c", i)]
-            for g in range(PASSES):
-                rows = slice(g * P, (g + 1) * P)
-                nc.tensor.matmul_mx(
-                    out=head_of[e][:, slot, :],
-                    lhsT=codes[:, rows].bitcast(FP8X4),
-                    lhsT_scale=plane[:, rows],
-                    rhs=w4_codes[:, PASSES * e + g, :].bitcast(FP8X4),
-                    rhs_scale=w4_planes[:, PASSES * e + g, :],
-                    start=(g == 0),
-                    stop=(g == PASSES - 1),
-                )
-
-        def add_b4(i):
-            e = i // UNITS_PER_MEMBER
-            n = (i % UNITS_PER_MEMBER) % GROUP + 1
-            nc.vector.tensor_tensor(
-                out=results[:, :, i + 1 - n : i + 1, :].rearrange("p h j o -> p j h o"),
-                in0=head_of[e][:, 0:n, :].rearrange("p j (h o) -> p j h o", h=2),
-                in1=shift[:, e, :].rearrange("p (h o) -> p h o", h=2).unsqueeze(1).to_broadcast([P, n, 2, OUT]),
-                op=ALU.add,
-            )
 
         clipped_of = {}
         tanh_of = {}
 
-        def begin_bounds(e):
-            units = slice(e * UNITS_PER_MEMBER, (e + 1) * UNITS_PER_MEMBER)
+        with ExitStack() as main:
+            loads = main.enter_context(tc.tile_pool(name="loads", bufs=2))
+            work = main.enter_context(tc.tile_pool(name="work", bufs=2))
+            psum = main.enter_context(tc.psum_pool(name="psum", bufs=2))
+
+            h2_of = {}
+            w3_raw_of = {}
+            w3_of = {}
+            grouped_a_of = {}
+            turned_of = {}
+            codes_a_of = {}
+            sums_of = {}
+            rows_of = {}
+            folded_of = {}
+            codes_c_of = {}
+            head_of = {}
+            results_of = {}
+
+            def load_h2(m):
+                h2_of[m] = loads.tile([P, UNITS, HIDDEN], BF16, name="h2_%d" % m, tag="h2")
+                rows = h2[m].rearrange("(p j) k -> p j k", j=UNITS)
+                for j in range(UNITS):
+                    nc.sync.dma_start(out=h2_of[m][:, j, :], in_=rows[:, j, :])
+
+            def load_w3_pass(m, g):
+                nc.sync.dma_start(
+                    out=w3_raw_of[m][:, g, :].bitcast(I32),
+                    in_=w3_words[PASSES * m + g].rearrange("p n t -> p (n t)").bitcast(I32),
+                )
+
+            def load_w3_planes(a):
+                first = a * PLANES_PER_TILE
+                n_planes = min(PLANES_PER_TILE, n_passes - first)
+                for quadrant in range(4):
+                    nc.sync.dma_start(
+                        out=w3_planes_raw[32 * quadrant : 32 * quadrant + 4 * n_planes, a, :].bitcast(I32),
+                        in_=w3_scales[first : first + n_planes, 4 * quadrant : 4 * quadrant + 4, :].bitcast(I32),
+                    )
+
+            def new_w3_raw(m):
+                w3_raw_of[m] = loads.tile([P, PASSES, HIDDEN], U32, name="w3_raw_%d" % m, tag="w3_raw", bufs=1)
+
+            new_w3_raw(0)
+            load_w3_pass(0, 0)
+            load_w3_planes(0)
+            load_w3_pass(0, 1)
+            load_h2(0)
+            b3_view = b3.rearrange("e o (h r s t) -> s (e o h) r t", h=PASSES, s=STEPS, t=PACK)
+            for s in range(STEPS):
+                nc.sync.dma_start(
+                    out=b3_rows[s : MEMBERS * PASSES * STEPS : STEPS, :].rearrange("c (r t) -> c r t", t=PACK),
+                    in_=b3_view[s],
+                )
+            for a in range(1, n_plane_tiles):
+                load_w3_planes(a)
+            for quadrant in range(4):
+                nc.sync.dma_start(
+                    out=w4_planes[32 * quadrant : 32 * quadrant + 4, :, :].bitcast(I32),
+                    in_=w4_scales[:, 4 * quadrant : 4 * quadrant + 4, :].rearrange("c r n -> r c n").bitcast(I32),
+                )
             nc.sync.dma_start(
-                out=out_0[e].rearrange("(p j) o -> p (j o)", j=UNITS_PER_MEMBER),
-                in_=results[:, 0, units, :].rearrange("p j o -> p (j o)"),
+                out=w4_codes[:].bitcast(I32),
+                in_=w4_words.rearrange("c p n t -> p c (n t)").bitcast(I32),
             )
-            u = results[:, 1, units, :]
-            size = tail.tile([P, UNITS_PER_MEMBER, OUT], F32, name="size_%d" % e, tag="size")
-            nc.vector.scalar_tensor_tensor(out=size[:], in0=u, scalar=-1.0, in1=u, op0=ALU.mult, op1=ALU.max)
-            clipped = tail.tile([P, UNITS_PER_MEMBER, OUT], F32, name="clipped_%d" % e, tag="clipped", bufs=MEMBERS)
-            nc.vector.scalar_tensor_tensor(
-                out=clipped[:],
-                in0=u,
-                scalar=0.0,
-                in1=span[:].unsqueeze(1).to_broadcast([P, UNITS_PER_MEMBER, OUT]),
-                op0=ALU.min,
-                op1=ALU.add,
+            nc.sync.dma_start(
+                out=b4_all[:].rearrange("p e n -> p (e n)"),
+                in_=b4.rearrange("e o n -> (e o n)").partition_broadcast(P),
             )
-            tanh = tail.tile([P, UNITS_PER_MEMBER, OUT], F32, name="tanh_%d" % e, tag="tanh", bufs=MEMBERS)
-            nc.scalar.activation(out=tanh[:], in_=size[:], func=ACT.Tanh, scale=0.5)
-            clipped_of[e] = clipped
-            tanh_of[e] = tanh
+            nc.sync.dma_start(out=max_lv[:], in_=max_logvar[0, :].partition_broadcast(P))
+            nc.sync.dma_start(out=min_lv[:], in_=min_logvar[0, :].partition_broadcast(P))
 
-        for r in range(-LEAD_A, UNITS + LAG_D):
-            unit_a = r + LEAD_A
-            unit_c = r - LAG_C
-            unit_d = r - LAG_D
-            unit_s = r - LAG_SILU
-            if 0 <= r < UNITS and r % UNITS_PER_MEMBER == 0 and r // UNITS_PER_MEMBER + 2 < MEMBERS:
-                load_member(r // UNITS_PER_MEMBER + 2)
+            def sort_w3(m):
+                w3_of[m] = work.tile([P, PASSES, HIDDEN], U32, name="w3_%d" % m, tag="w3", align_bytes=64)
+                if (PASSES * m) % PLANES_PER_TILE == 0:
+                    a = (PASSES * m) // PLANES_PER_TILE
+                    for h in range(PASSES):
+                        cols = slice(h * K_PASS, (h + 1) * K_PASS)
+                        nc.vector.tensor_copy(
+                            out=w3_planes[:, a, cols].bitcast(I32).rearrange("p (s r) -> p s r", s=STEPS),
+                            in_=w3_planes_raw[:, a, cols].bitcast(I32).rearrange("p (r s) -> p s r", s=STEPS),
+                        )
+                for g in range(PASSES):
+                    for h in range(PASSES):
+                        cols = slice(h * K_PASS, (h + 1) * K_PASS)
+                        nc.vector.tensor_copy(
+                            out=w3_of[m][:, g, cols].bitcast(I32).rearrange("p (s r t) -> p s r t", s=STEPS, t=PACK),
+                            in_=w3_raw_of[m][:, g, cols].bitcast(I32).rearrange("p (r s t) -> p s r t", s=STEPS, t=PACK),
+                        )
 
-            if 0 <= unit_c < UNITS:
-                transpose_words("c", unit_c, h3_of[unit_c][:].bitcast(F32), 1)
-            if unit_a < UNITS:
-                e_a = unit_a // UNITS_PER_MEMBER
-                transpose_words("a", unit_a, h2_of[e_a][:, unit_a % UNITS_PER_MEMBER, :].bitcast(F32), 2)
-            if 0 <= unit_d < UNITS:
-                second_matmul(unit_d)
-            if 0 <= r < UNITS:
-                first_matmul(r)
+            def chunk_of_unit(j):
+                return [i for i in range(len(CHUNKS)) if CHUNKS[i][0] <= j * P < CHUNKS[i][1]][0]
 
-            grouped_c = copy_out("c", unit_c) if 0 <= unit_c < UNITS else None
-            grouped_a = copy_out("a", unit_a) if unit_a < UNITS else None
-            if 0 <= unit_s < UNITS:
-                silu(unit_s)
+            def transpose_h2(m, j):
+                words = h2_of[m][:, j, :].bitcast(F32)
+                bank = psum.tile([P, PASSES * 2, P], F32, name="turned_%d_%d" % (m, j), tag="turned")
+                for g in range(PASSES):
+                    for u in range(2):
+                        nc.tensor.transpose(
+                            out=bank[:, 2 * g + u, :],
+                            in_=words[:, 256 * g + u : 256 * (g + 1) : 2],
+                            identity=ident[:],
+                        )
+                turned_of[(m, j)] = bank
 
-            if grouped_c is not None:
-                quantise("c", unit_c, grouped_c)
-            if grouped_a is not None:
-                quantise("a", unit_a, grouped_a)
-            if 0 <= unit_d < UNITS:
-                place = unit_d % UNITS_PER_MEMBER
-                if place % GROUP == GROUP - 1 or place == UNITS_PER_MEMBER - 1:
-                    add_b4(unit_d)
-                if place == UNITS_PER_MEMBER - 1:
-                    begin_bounds(unit_d // UNITS_PER_MEMBER)
-            if 0 <= r < UNITS:
-                add_b3(r)
+            def copy_out_h2(m, j):
+                i = chunk_of_unit(j)
+                first, last = CHUNKS[i]
+                if j * P == first:
+                    grouped_a_of[(m, i)] = work.tile(
+                        [P, PASSES, last - first, PACK], BF16, name="grouped_a_%d_%d" % (m, i), tag="grouped_a", align_bytes=64
+                    )
+                nc.scalar.copy(
+                    out=grouped_a_of[(m, i)][:, :, j * P - first : (j + 1) * P - first, :].bitcast(F32),
+                    in_=turned_of[(m, j)][:].rearrange("p (g u) r -> p g r u", u=2),
+                )
 
-        shape = [P, UNITS_PER_MEMBER, OUT]
+            def quantise_h2(m, i):
+                first, last = CHUNKS[i]
+                if i == 0:
+                    codes = work.tile([P, PASSES, BATCH], U32, name="codes_a_%d" % m, tag="codes_a", align_bytes=64)
+                    plane = work.tile([P, PASSES, BATCH], U8, name="plane_a_%d" % m, tag="plane_a", align_bytes=64)
+                    codes_a_of[m] = (codes, plane)
+                codes, plane = codes_a_of[m]
+                for g in range(PASSES):
+                    nc.vector.quantize_mx(
+                        out=codes[:, g, first:last].bitcast(FP8X4),
+                        scales=plane[:, g, first:last],
+                        in_=grouped_a_of[(m, i)][:, g, :, :].rearrange("p r t -> p (r t)"),
+                    )
+
+            def first_matmul(m, s, h):
+                codes, plane = codes_a_of[m]
+                tile_cols = slice((h * STEPS + s) * P, (h * STEPS + s + 1) * P)
+                wide = psum.tile([P, BANK], F32, name="wide_%d_%d_%d" % (m, s, h), tag="wide")
+                narrow = psum.tile([P, BATCH - BANK], F32, name="narrow_%d_%d_%d" % (m, s, h), tag="narrow")
+                for first, last in CHUNKS:
+                    sums = wide[:] if first == 0 else narrow[:, first - BANK : last - BANK]
+                    for g in range(PASSES):
+                        c = PASSES * m + g
+                        nc.tensor.matmul_mx(
+                            out=sums,
+                            lhsT=w3_of[m][:, g, tile_cols].bitcast(FP8X4),
+                            lhsT_scale=w3_planes[4 * (c % PLANES_PER_TILE) : P, c // PLANES_PER_TILE, tile_cols],
+                            rhs=codes[:, g, first:last].bitcast(FP8X4),
+                            rhs_scale=plane[:, g, first:last],
+                            start=(g == 0),
+                            stop=(g == PASSES - 1),
+                        )
+                sums_of[(m, s, h)] = (wide, narrow)
+
+            def silu(m, s, h):
+                if h == 0:
+                    rows_of[(m, s)] = work.tile([P, PASSES, BATCH], BF16, name="rows_%d_%d" % (m, s), tag="rows", bufs=4)
+                wide, narrow = sums_of[(m, s, h)]
+                column = (m * PASSES + h) * STEPS + s
+                bias = b3_columns[:, column : column + 1]
+                nc.scalar.activation(out=rows_of[(m, s)][:, h, 0:BANK], in_=wide[:], func=ACT.Silu, bias=bias)
+                nc.scalar.activation(out=rows_of[(m, s)][:, h, BANK:BATCH], in_=narrow[:], func=ACT.Silu, bias=bias)
+
+            def fold(m, s):
+                if s == 0:
+                    folded_of[m] = work.tile([P, PASSES, PACK, BATCH], BF16, name="folded_%d" % m, tag="folded")
+                for t in range(PACK):
+                    nc.sync.dma_start(out=folded_of[m][s:P:STEPS, :, t, :], in_=rows_of[(m, s)][t:P:PACK, :, :])
+
+            def quantise_h3(m, i):
+                first, last = CHUNKS[i]
+                if i == 0:
+                    codes = work.tile([P, PASSES, BATCH], U32, name="codes_c_%d" % m, tag="codes_c", bufs=1, align_bytes=64)
+                    plane = work.tile([P, PASSES, BATCH], U8, name="plane_c_%d" % m, tag="plane_c", bufs=1, align_bytes=64)
+                    codes_c_of[m] = (codes, plane)
+                codes, plane = codes_c_of[m]
+                grouped = []
+                for g in range(PASSES):
+                    grouped.append(
+                        work.tile([P, last - first, PACK], BF16, name="grouped_c_%d_%d_%d" % (m, i, g), tag="grouped_c", bufs=3, align_bytes=64)
+                    )
+                    nc.vector.tensor_copy(
+                        out=grouped[g][:], in_=folded_of[m][:, g, :, first:last].rearrange("p t r -> p r t")
+                    )
+                for g in range(PASSES):
+                    nc.vector.quantize_mx(
+                        out=codes[:, g, first:last].bitcast(FP8X4),
+                        scales=plane[:, g, first:last],
+                        in_=grouped[g][:].rearrange("p r t -> p (r t)"),
+                    )
+
+            def second_matmul(m, group):
+                codes, plane = codes_c_of[m]
+                first, last = HEAD_GROUPS[group]
+                head_of[m] = psum.tile([P, BANK // OUT2, OUT2], F32, name="head_%d_%d" % (m, group), tag="head")
+                for j in range(first, last):
+                    for g in range(PASSES):
+                        nc.tensor.matmul_mx(
+                            out=head_of[m][:, j - first, :],
+                            lhsT=codes[:, g, j * P : (j + 1) * P].bitcast(FP8X4),
+                            lhsT_scale=plane[:, g, j * P : (j + 1) * P],
+                            rhs=w4_codes[:, PASSES * m + g, :].bitcast(FP8X4),
+                            rhs_scale=w4_planes[:, PASSES * m + g, :],
+                            start=(g == 0),
+                            stop=(g == PASSES - 1),
+                        )
+
+            def add_b4(m, group):
+                first, last = HEAD_GROUPS[group]
+                if group == 0:
+                    results_of[m] = work.tile([P, 2, UNITS, OUT], F32, name="results_%d" % m, tag="results")
+                nc.vector.tensor_tensor(
+                    out=results_of[m][:, :, first:last, :].rearrange("p h j o -> p j h o"),
+                    in0=head_of[m][:, 0 : last - first, :].rearrange("p j (h o) -> p j h o", h=2),
+                    in1=shift[:, m, :].rearrange("p (h o) -> p h o", h=2).unsqueeze(1).to_broadcast([P, last - first, 2, OUT]),
+                    op=ALU.add,
+                )
+
+            def begin_bounds(m):
+                nc.sync.dma_start(
+                    out=out_0[m].rearrange("(p j) o -> p (j o)", j=UNITS),
+                    in_=results_of[m][:, 0, :, :].rearrange("p j o -> p (j o)"),
+                )
+                u = results_of[m][:, 1, :, :]
+                size = work.tile(member_shape, F32, name="size_%d" % m, tag="size")
+                nc.vector.scalar_tensor_tensor(out=size[:], in0=u, scalar=-1.0, in1=u, op0=ALU.mult, op1=ALU.max)
+                clipped_of[m] = bounds.tile(member_shape, F32, name="clipped_%d" % m, tag="clipped")
+                nc.vector.scalar_tensor_tensor(
+                    out=clipped_of[m][:],
+                    in0=u,
+                    scalar=0.0,
+                    in1=span[:].unsqueeze(1).to_broadcast(member_shape),
+                    op0=ALU.min,
+                    op1=ALU.add,
+                )
+                tanh_of[m] = bounds.tile(member_shape, F32, name="tanh_%d" % m, tag="tanh")
+                nc.scalar.activation(out=tanh_of[m][:], in_=size[:], func=ACT.Tanh, scale=0.5)
+
+            for e in range(-1, MEMBERS + 1):
+                ahead = e + 1
+                behind = e - 1
+                does_a = ahead < MEMBERS
+                does_b = 0 <= e < MEMBERS
+                does_cd = 0 <= behind
+                for s in range(STEPS):
+                    units = range(s * UNITS_PER_STEP, min((s + 1) * UNITS_PER_STEP, UNITS))
+                    if s == 0 and e + 2 < MEMBERS:
+                        load_h2(e + 2)
+                    if s == 1 and e + 2 < MEMBERS:
+                        new_w3_raw(e + 2)
+                        for g in range(PASSES):
+                            load_w3_pass(e + 2, g)
+
+                    if does_a:
+                        for j in units:
+                            transpose_h2(ahead, j)
+                    if e == -1 and s == STEPS - 1:
+                        nc.vector.tensor_copy(out=b3_rows_f32[:], in_=b3_rows[:])
+                        b3_turned = psum.tile([P, PASSES * 2, P], F32, name="b3_turned", tag="turned")
+                        nc.tensor.transpose(out=b3_turned[:, 0, :], in_=b3_rows_f32[:], identity=ident[:])
+                    if does_b:
+                        for h in range(PASSES):
+                            first_matmul(e, s, h)
+                    if does_cd and s >= STEPS - len(HEAD_GROUPS):
+                        second_matmul(behind, s - (STEPS - len(HEAD_GROUPS)))
+
+                    if does_a:
+                        for j in units:
+                            copy_out_h2(ahead, j)
+                    if does_b:
+                        for h in range(PASSES):
+                            silu(e, s, h)
+                        fold(e, s)
+
+                    if e == -1 and s == STEPS - 1:
+                        nc.vector.tensor_copy(out=b3_columns[:], in_=b3_turned[:, 0, 0 : MEMBERS * PASSES * STEPS])
+                    if e == 0 and s == 0:
+                        nc.vector.tensor_copy(out=shift[:, :, 0:OUT], in_=b4_all[:, :, 0:OUT])
+                        nc.vector.tensor_tensor(
+                            out=shift[:, :, OUT:OUT2],
+                            in0=b4_all[:, :, OUT:OUT2],
+                            in1=max_lv[:].unsqueeze(1).to_broadcast([P, MEMBERS, OUT]),
+                            op=ALU.subtract,
+                        )
+                        nc.vector.tensor_tensor(out=span[:], in0=max_lv[:], in1=min_lv[:], op=ALU.subtract)
+                    if s == 0 and does_a:
+                        sort_w3(ahead)
+                    if does_cd and s < len(CHUNKS):
+                        quantise_h3(behind, s)
+                    if does_a:
+                        for i in range(len(CHUNKS)):
+                            if (CHUNKS[i][1] // P - 1) // UNITS_PER_STEP == s:
+                                quantise_h2(ahead, i)
+                    if does_cd and s >= STEPS - len(HEAD_GROUPS):
+                        add_b4(behind, s - (STEPS - len(HEAD_GROUPS)))
+                    if does_cd and s == STEPS - 1:
+                        begin_bounds(behind)
+
+        tail = whole.enter_context(tc.tile_pool(name="tail", bufs=2))
         size2_of = {}
         floor_of = {}
         for e in range(MEMBERS):
-            log1 = tail.tile(shape, F32, name="log1_%d" % e, tag="log1")
+            log1 = tail.tile(member_shape, F32, name="log1_%d" % e, tag="log1")
             nc.scalar.activation(out=log1[:], in_=tanh_of[e][:], func=ACT.Ln, scale=0.5, bias=half[:])
-            v = tail.tile(shape, F32, name="v_%d" % e, tag="v")
+            v = tail.tile(member_shape, F32, name="v_%d" % e, tag="v")
             nc.vector.tensor_tensor(out=v[:], in0=clipped_of[e][:], in1=log1[:], op=ALU.add)
-            size2_of[e] = tail.tile(shape, F32, name="size2_%d" % e, tag="size2", bufs=MEMBERS)
+            size2_of[e] = tail.tile(member_shape, F32, name="size2_%d" % e, tag="size2", bufs=MEMBERS)
             nc.vector.scalar_tensor_tensor(
                 out=size2_of[e][:], in0=v[:], scalar=-1.0, in1=v[:], op0=ALU.mult, op1=ALU.max
             )
-            floor_of[e] = tail.tile(shape, F32, name="floor_%d" % e, tag="floor", bufs=MEMBERS)
+            floor_of[e] = tail.tile(member_shape, F32, name="floor_%d" % e, tag="floor", bufs=MEMBERS)
             nc.vector.scalar_tensor_tensor(
                 out=floor_of[e][:],
                 in0=v[:],
                 scalar=0.0,
-                in1=min_lv[:].unsqueeze(1).to_broadcast(shape),
+                in1=min_lv[:].unsqueeze(1).to_broadcast(member_shape),
                 op0=ALU.max,
                 op1=ALU.add,
             )
         tanh2_of = {}
         for e in range(MEMBERS):
-            tanh2_of[e] = tail.tile(shape, F32, name="tanh2_%d" % e, tag="tanh2", bufs=MEMBERS)
+            tanh2_of[e] = tail.tile(member_shape, F32, name="tanh2_%d" % e, tag="tanh2", bufs=MEMBERS)
             nc.scalar.activation(out=tanh2_of[e][:], in_=size2_of[e][:], func=ACT.Tanh, scale=0.5)
         for e in range(MEMBERS):
-            log2 = tail.tile(shape, F32, name="log2_%d" % e, tag="log2")
+            log2 = tail.tile(member_shape, F32, name="log2_%d" % e, tag="log2")
             nc.scalar.activation(out=log2[:], in_=tanh2_of[e][:], func=ACT.Ln, scale=0.5, bias=half[:])
-            logvar = tail.tile(shape, F32, name="logvar_%d" % e, tag="logvar")
+            logvar = tail.tile(member_shape, F32, name="logvar_%d" % e, tag="logvar")
             nc.vector.tensor_tensor(out=logvar[:], in0=floor_of[e][:], in1=log2[:], op=ALU.subtract)
             nc.sync.dma_start(
-                out=out_1[e].rearrange("(p j) o -> p (j o)", j=UNITS_PER_MEMBER),
+                out=out_1[e].rearrange("(p j) o -> p (j o)", j=UNITS),
                 in_=logvar[:].rearrange("p j o -> p (j o)"),
             )

@@ -45,10 +45,12 @@ def tile_ensembledynamicsmodel_pa_t_e_kernel(
 
         ident = keep.tile([P, P], F32)
         make_identity(nc, ident[:])
-        half = keep.tile([P, 1], F32)
-        nc.vector.memset(half[:], 0.5)
+        one = keep.tile([P, 1], F32)
+        nc.vector.memset(one[:], 1.0)
+        two = keep.tile([P, 1], F32)
+        nc.vector.memset(two[:], 2.0)
         warm = keep.tile([P, 1], F32)
-        nc.scalar.activation(out=warm[:], in_=half[:], func=ACT.Silu)
+        nc.scalar.activation(out=warm[:], in_=one[:], func=ACT.Silu)
 
         n_passes = MEMBERS * PASSES
         n_plane_tiles = (n_passes + PLANES_PER_TILE - 1) // PLANES_PER_TILE
@@ -69,8 +71,9 @@ def tile_ensembledynamicsmodel_pa_t_e_kernel(
         shift = keep.tile([P, MEMBERS, OUT2], F32)
         span = keep.tile([P, OUT], F32)
 
-        clipped_of = {}
-        tanh_of = {}
+        product_of = {}
+        abs_tau_of = {}
+        floor_of = {}
 
         with ExitStack() as main:
             loads = main.enter_context(tc.tile_pool(name="loads", bufs=2))
@@ -86,21 +89,25 @@ def tile_ensembledynamicsmodel_pa_t_e_kernel(
             sums_of = {}
             rows_of = {}
             folded_of = {}
+            grouped_c_of = {}
             codes_c_of = {}
             head_of = {}
             results_of = {}
 
-            def load_h2(m):
-                h2_of[m] = loads.tile([P, UNITS, HIDDEN], BF16, name="h2_%d" % m, tag="h2")
+            def load_h2(m, units):
+                if units[0] == 0:
+                    h2_of[m] = loads.tile([P, UNITS, HIDDEN], BF16, name="h2_%d" % m, tag="h2")
                 rows = h2[m].rearrange("(p j) k -> p j k", j=UNITS)
-                for j in range(UNITS):
+                for j in units:
                     nc.sync.dma_start(out=h2_of[m][:, j, :], in_=rows[:, j, :])
 
-            def load_w3_pass(m, g):
-                nc.sync.dma_start(
-                    out=w3_raw_of[m][:, g, :].bitcast(I32),
-                    in_=w3_words[PASSES * m + g].rearrange("p n t -> p (n t)").bitcast(I32),
-                )
+            def load_w3_half(m, h):
+                for g in range(PASSES):
+                    words = w3_words[PASSES * m + g].rearrange("p n t -> p (n t)")
+                    nc.sync.dma_start(
+                        out=w3_raw_of[m][:, g, h * K_PASS : (h + 1) * K_PASS].bitcast(I32),
+                        in_=words[:, h * K_PASS * PACK : (h + 1) * K_PASS * PACK].bitcast(I32),
+                    )
 
             def load_w3_planes(a):
                 first = a * PLANES_PER_TILE
@@ -115,10 +122,11 @@ def tile_ensembledynamicsmodel_pa_t_e_kernel(
                 w3_raw_of[m] = loads.tile([P, PASSES, HIDDEN], U32, name="w3_raw_%d" % m, tag="w3_raw", bufs=1)
 
             new_w3_raw(0)
-            load_w3_pass(0, 0)
+            load_w3_half(0, 0)
             load_w3_planes(0)
-            load_w3_pass(0, 1)
-            load_h2(0)
+            load_h2(0, range(0, CHUNKS[0][1] // P))
+            load_w3_half(0, 1)
+            load_h2(0, range(CHUNKS[0][1] // P, UNITS))
             b3_view = b3.rearrange("e o (h r s t) -> s (e o h) r t", h=PASSES, s=STEPS, t=PACK)
             for s in range(STEPS):
                 nc.sync.dma_start(
@@ -143,26 +151,28 @@ def tile_ensembledynamicsmodel_pa_t_e_kernel(
             nc.sync.dma_start(out=max_lv[:], in_=max_logvar[0, :].partition_broadcast(P))
             nc.sync.dma_start(out=min_lv[:], in_=min_logvar[0, :].partition_broadcast(P))
 
-            def sort_w3(m):
-                w3_of[m] = work.tile([P, PASSES, HIDDEN], U32, name="w3_%d" % m, tag="w3", align_bytes=64)
+            def sort_w3(m, h):
+                if h == 0:
+                    w3_of[m] = work.tile([P, PASSES, HIDDEN], U32, name="w3_%d" % m, tag="w3", align_bytes=64)
+                cols = slice(h * K_PASS, (h + 1) * K_PASS)
                 if (PASSES * m) % PLANES_PER_TILE == 0:
                     a = (PASSES * m) // PLANES_PER_TILE
-                    for h in range(PASSES):
-                        cols = slice(h * K_PASS, (h + 1) * K_PASS)
-                        nc.vector.tensor_copy(
-                            out=w3_planes[:, a, cols].bitcast(I32).rearrange("p (s r) -> p s r", s=STEPS),
-                            in_=w3_planes_raw[:, a, cols].bitcast(I32).rearrange("p (r s) -> p s r", s=STEPS),
-                        )
+                    nc.vector.tensor_copy(
+                        out=w3_planes[:, a, cols].bitcast(I32).rearrange("p (s r) -> p s r", s=STEPS),
+                        in_=w3_planes_raw[:, a, cols].bitcast(I32).rearrange("p (r s) -> p s r", s=STEPS),
+                    )
                 for g in range(PASSES):
-                    for h in range(PASSES):
-                        cols = slice(h * K_PASS, (h + 1) * K_PASS)
-                        nc.vector.tensor_copy(
-                            out=w3_of[m][:, g, cols].bitcast(I32).rearrange("p (s r t) -> p s r t", s=STEPS, t=PACK),
-                            in_=w3_raw_of[m][:, g, cols].bitcast(I32).rearrange("p (r s t) -> p s r t", s=STEPS, t=PACK),
-                        )
+                    nc.vector.tensor_copy(
+                        out=w3_of[m][:, g, cols].bitcast(I32).rearrange("p (s r t) -> p s r t", s=STEPS, t=PACK),
+                        in_=w3_raw_of[m][:, g, cols].bitcast(I32).rearrange("p (r s t) -> p s r t", s=STEPS, t=PACK),
+                    )
 
             def chunk_of_unit(j):
                 return [i for i in range(len(CHUNKS)) if CHUNKS[i][0] <= j * P < CHUNKS[i][1]][0]
+
+            def code_column(i, g):
+                first, last = CHUNKS[i]
+                return PASSES * first + g * (last - first)
 
             def transpose_h2(m, j):
                 words = h2_of[m][:, j, :].bitcast(F32)
@@ -191,32 +201,33 @@ def tile_ensembledynamicsmodel_pa_t_e_kernel(
             def quantise_h2(m, i):
                 first, last = CHUNKS[i]
                 if i == 0:
-                    codes = work.tile([P, PASSES, BATCH], U32, name="codes_a_%d" % m, tag="codes_a", align_bytes=64)
-                    plane = work.tile([P, PASSES, BATCH], U8, name="plane_a_%d" % m, tag="plane_a", align_bytes=64)
+                    codes = work.tile([P, PASSES * BATCH], U32, name="codes_a_%d" % m, tag="codes_a", align_bytes=64)
+                    plane = work.tile([P, PASSES * BATCH], U8, name="plane_a_%d" % m, tag="plane_a", align_bytes=64)
                     codes_a_of[m] = (codes, plane)
                 codes, plane = codes_a_of[m]
-                for g in range(PASSES):
-                    nc.vector.quantize_mx(
-                        out=codes[:, g, first:last].bitcast(FP8X4),
-                        scales=plane[:, g, first:last],
-                        in_=grouped_a_of[(m, i)][:, g, :, :].rearrange("p r t -> p (r t)"),
-                    )
+                nc.vector.quantize_mx(
+                    out=codes[:, PASSES * first : PASSES * last].bitcast(FP8X4),
+                    scales=plane[:, PASSES * first : PASSES * last],
+                    in_=grouped_a_of[(m, i)][:].rearrange("p g r t -> p (g r t)"),
+                )
 
             def first_matmul(m, s, h):
                 codes, plane = codes_a_of[m]
                 tile_cols = slice((h * STEPS + s) * P, (h * STEPS + s + 1) * P)
                 wide = psum.tile([P, BANK], F32, name="wide_%d_%d_%d" % (m, s, h), tag="wide")
                 narrow = psum.tile([P, BATCH - BANK], F32, name="narrow_%d_%d_%d" % (m, s, h), tag="narrow")
-                for first, last in CHUNKS:
+                for i in range(len(CHUNKS)):
+                    first, last = CHUNKS[i]
                     sums = wide[:] if first == 0 else narrow[:, first - BANK : last - BANK]
                     for g in range(PASSES):
                         c = PASSES * m + g
+                        cols = slice(code_column(i, g), code_column(i, g) + last - first)
                         nc.tensor.matmul_mx(
                             out=sums,
                             lhsT=w3_of[m][:, g, tile_cols].bitcast(FP8X4),
                             lhsT_scale=w3_planes[4 * (c % PLANES_PER_TILE) : P, c // PLANES_PER_TILE, tile_cols],
-                            rhs=codes[:, g, first:last].bitcast(FP8X4),
-                            rhs_scale=plane[:, g, first:last],
+                            rhs=codes[:, cols].bitcast(FP8X4),
+                            rhs_scale=plane[:, cols],
                             start=(g == 0),
                             stop=(g == PASSES - 1),
                         )
@@ -237,38 +248,42 @@ def tile_ensembledynamicsmodel_pa_t_e_kernel(
                 for t in range(PACK):
                     nc.sync.dma_start(out=folded_of[m][s:P:STEPS, :, t, :], in_=rows_of[(m, s)][t:P:PACK, :, :])
 
+            def regroup_h3(m, i):
+                first, last = CHUNKS[i]
+                grouped_c_of[(m, i)] = work.tile(
+                    [P, PASSES, last - first, PACK], BF16, name="grouped_c_%d_%d" % (m, i), tag="grouped_c", align_bytes=64
+                )
+                for g in range(PASSES):
+                    nc.vector.tensor_copy(
+                        out=grouped_c_of[(m, i)][:, g, :, :].rearrange("p (c i) t -> p c t i", i=4),
+                        in_=folded_of[m][:, g, :, first:last].rearrange("p t (c i) -> p c t i", i=4),
+                    )
+
             def quantise_h3(m, i):
                 first, last = CHUNKS[i]
                 if i == 0:
-                    codes = work.tile([P, PASSES, BATCH], U32, name="codes_c_%d" % m, tag="codes_c", bufs=1, align_bytes=64)
-                    plane = work.tile([P, PASSES, BATCH], U8, name="plane_c_%d" % m, tag="plane_c", bufs=1, align_bytes=64)
+                    codes = work.tile([P, PASSES * BATCH], U32, name="codes_c_%d" % m, tag="codes_c", bufs=1, align_bytes=64)
+                    plane = work.tile([P, PASSES * BATCH], U8, name="plane_c_%d" % m, tag="plane_c", bufs=1, align_bytes=64)
                     codes_c_of[m] = (codes, plane)
                 codes, plane = codes_c_of[m]
-                grouped = []
-                for g in range(PASSES):
-                    grouped.append(
-                        work.tile([P, last - first, PACK], BF16, name="grouped_c_%d_%d_%d" % (m, i, g), tag="grouped_c", bufs=3, align_bytes=64)
-                    )
-                    nc.vector.tensor_copy(
-                        out=grouped[g][:], in_=folded_of[m][:, g, :, first:last].rearrange("p t r -> p r t")
-                    )
-                for g in range(PASSES):
-                    nc.vector.quantize_mx(
-                        out=codes[:, g, first:last].bitcast(FP8X4),
-                        scales=plane[:, g, first:last],
-                        in_=grouped[g][:].rearrange("p r t -> p (r t)"),
-                    )
+                nc.vector.quantize_mx(
+                    out=codes[:, PASSES * first : PASSES * last].bitcast(FP8X4),
+                    scales=plane[:, PASSES * first : PASSES * last],
+                    in_=grouped_c_of[(m, i)][:].rearrange("p g r t -> p (g r t)"),
+                )
 
             def second_matmul(m, group):
                 codes, plane = codes_c_of[m]
                 first, last = HEAD_GROUPS[group]
                 head_of[m] = psum.tile([P, BANK // OUT2, OUT2], F32, name="head_%d_%d" % (m, group), tag="head")
                 for j in range(first, last):
+                    i = chunk_of_unit(j)
                     for g in range(PASSES):
+                        start = code_column(i, g) + j * P - CHUNKS[i][0]
                         nc.tensor.matmul_mx(
                             out=head_of[m][:, j - first, :],
-                            lhsT=codes[:, g, j * P : (j + 1) * P].bitcast(FP8X4),
-                            lhsT_scale=plane[:, g, j * P : (j + 1) * P],
+                            lhsT=codes[:, start : start + P].bitcast(FP8X4),
+                            lhsT_scale=plane[:, start : start + P],
                             rhs=w4_codes[:, PASSES * m + g, :].bitcast(FP8X4),
                             rhs_scale=w4_planes[:, PASSES * m + g, :],
                             start=(g == 0),
@@ -292,19 +307,52 @@ def tile_ensembledynamicsmodel_pa_t_e_kernel(
                     in_=results_of[m][:, 0, :, :].rearrange("p j o -> p (j o)"),
                 )
                 u = results_of[m][:, 1, :, :]
-                size = work.tile(member_shape, F32, name="size_%d" % m, tag="size")
-                nc.vector.scalar_tensor_tensor(out=size[:], in0=u, scalar=-1.0, in1=u, op0=ALU.mult, op1=ALU.max)
-                clipped_of[m] = bounds.tile(member_shape, F32, name="clipped_%d" % m, tag="clipped")
+                minus_size = work.tile(member_shape, F32, name="minus_size_%d" % m, tag="minus_size")
+                nc.vector.scalar_tensor_tensor(out=minus_size[:], in0=u, scalar=-1.0, in1=u, op0=ALU.mult, op1=ALU.min)
+                c = work.tile(member_shape, F32, name="c_%d" % m, tag="c")
                 nc.vector.scalar_tensor_tensor(
-                    out=clipped_of[m][:],
+                    out=c[:],
                     in0=u,
                     scalar=0.0,
                     in1=span[:].unsqueeze(1).to_broadcast(member_shape),
                     op0=ALU.min,
                     op1=ALU.add,
                 )
-                tanh_of[m] = bounds.tile(member_shape, F32, name="tanh_%d" % m, tag="tanh")
-                nc.scalar.activation(out=tanh_of[m][:], in_=size[:], func=ACT.Tanh, scale=0.5)
+                eta = work.tile(member_shape, F32, name="eta_%d" % m, tag="eta")
+                nc.scalar.activation(out=eta[:], in_=minus_size[:], func=ACT.Tanh, scale=0.5)
+                tau = work.tile(member_shape, F32, name="tau_%d" % m, tag="tau")
+                nc.scalar.activation(out=tau[:], in_=c[:], func=ACT.Tanh, scale=0.5)
+                floor_of[m] = bounds.tile(member_shape, F32, name="floor_%d" % m, tag="floor")
+                nc.vector.scalar_tensor_tensor(
+                    out=floor_of[m][:],
+                    in0=c[:],
+                    scalar=0.0,
+                    in1=min_lv[:].unsqueeze(1).to_broadcast(member_shape),
+                    op0=ALU.max,
+                    op1=ALU.add,
+                )
+                one_plus_eta = work.tile(member_shape, F32, name="one_plus_eta_%d" % m, tag="one_plus_eta")
+                nc.vector.tensor_scalar_add(out=one_plus_eta[:], in0=eta[:], scalar1=1.0)
+                product_of[m] = bounds.tile(member_shape, F32, name="product_%d" % m, tag="product")
+                nc.vector.scalar_tensor_tensor(
+                    out=product_of[m][:], in0=tau[:], scalar=1.0, in1=one_plus_eta[:], op0=ALU.add, op1=ALU.mult
+                )
+                abs_tau_of[m] = bounds.tile(member_shape, F32, name="abs_tau_%d" % m, tag="abs_tau")
+                nc.vector.scalar_tensor_tensor(
+                    out=abs_tau_of[m][:], in0=tau[:], scalar=-1.0, in1=tau[:], op0=ALU.mult, op1=ALU.max
+                )
+
+            def take_logs(m):
+                nc.scalar.activation(out=product_of[m][:], in_=product_of[m][:], func=ACT.Ln, scale=-0.5, bias=two[:])
+                nc.scalar.activation(out=abs_tau_of[m][:], in_=abs_tau_of[m][:], func=ACT.Ln, bias=one[:])
+
+            def finish_bounds(m):
+                nc.vector.tensor_tensor(out=floor_of[m][:], in0=floor_of[m][:], in1=product_of[m][:], op=ALU.add)
+                nc.vector.tensor_tensor(out=floor_of[m][:], in0=floor_of[m][:], in1=abs_tau_of[m][:], op=ALU.subtract)
+                nc.sync.dma_start(
+                    out=out_1[m].rearrange("(p j) o -> p (j o)", j=UNITS),
+                    in_=floor_of[m][:].rearrange("p j o -> p (j o)"),
+                )
 
             for e in range(-1, MEMBERS + 1):
                 ahead = e + 1
@@ -315,11 +363,11 @@ def tile_ensembledynamicsmodel_pa_t_e_kernel(
                 for s in range(STEPS):
                     units = range(s * UNITS_PER_STEP, min((s + 1) * UNITS_PER_STEP, UNITS))
                     if s == 0 and e + 2 < MEMBERS:
-                        load_h2(e + 2)
-                    if s == 1 and e + 2 < MEMBERS:
+                        load_h2(e + 2, range(UNITS))
+                    if s == 2 and e + 2 < MEMBERS:
                         new_w3_raw(e + 2)
-                        for g in range(PASSES):
-                            load_w3_pass(e + 2, g)
+                        for h in range(PASSES):
+                            load_w3_half(e + 2, h)
 
                     if does_a:
                         for j in units:
@@ -341,6 +389,9 @@ def tile_ensembledynamicsmodel_pa_t_e_kernel(
                         for h in range(PASSES):
                             silu(e, s, h)
                         fold(e, s)
+                    if e == MEMBERS and s == 0:
+                        for m in range(MEMBERS - 1):
+                            take_logs(m)
 
                     if e == -1 and s == STEPS - 1:
                         nc.vector.tensor_copy(out=b3_columns[:], in_=b3_turned[:, 0, 0 : MEMBERS * PASSES * STEPS])
@@ -353,50 +404,24 @@ def tile_ensembledynamicsmodel_pa_t_e_kernel(
                             op=ALU.subtract,
                         )
                         nc.vector.tensor_tensor(out=span[:], in0=max_lv[:], in1=min_lv[:], op=ALU.subtract)
-                    if s == 0 and does_a:
-                        sort_w3(ahead)
+                    if does_a and s == 0:
+                        sort_w3(ahead, 0)
                     if does_cd and s < len(CHUNKS):
-                        quantise_h3(behind, s)
+                        regroup_h3(behind, s)
                     if does_a:
                         for i in range(len(CHUNKS)):
                             if (CHUNKS[i][1] // P - 1) // UNITS_PER_STEP == s:
                                 quantise_h2(ahead, i)
+                    if does_a and s == 1:
+                        sort_w3(ahead, 1)
+                    if does_cd and s < len(CHUNKS):
+                        quantise_h3(behind, s)
                     if does_cd and s >= STEPS - len(HEAD_GROUPS):
                         add_b4(behind, s - (STEPS - len(HEAD_GROUPS)))
                     if does_cd and s == STEPS - 1:
                         begin_bounds(behind)
 
-        tail = whole.enter_context(tc.tile_pool(name="tail", bufs=2))
-        size2_of = {}
-        floor_of = {}
-        for e in range(MEMBERS):
-            log1 = tail.tile(member_shape, F32, name="log1_%d" % e, tag="log1")
-            nc.scalar.activation(out=log1[:], in_=tanh_of[e][:], func=ACT.Ln, scale=0.5, bias=half[:])
-            v = tail.tile(member_shape, F32, name="v_%d" % e, tag="v")
-            nc.vector.tensor_tensor(out=v[:], in0=clipped_of[e][:], in1=log1[:], op=ALU.add)
-            size2_of[e] = tail.tile(member_shape, F32, name="size2_%d" % e, tag="size2", bufs=MEMBERS)
-            nc.vector.scalar_tensor_tensor(
-                out=size2_of[e][:], in0=v[:], scalar=-1.0, in1=v[:], op0=ALU.mult, op1=ALU.max
-            )
-            floor_of[e] = tail.tile(member_shape, F32, name="floor_%d" % e, tag="floor", bufs=MEMBERS)
-            nc.vector.scalar_tensor_tensor(
-                out=floor_of[e][:],
-                in0=v[:],
-                scalar=0.0,
-                in1=min_lv[:].unsqueeze(1).to_broadcast(member_shape),
-                op0=ALU.max,
-                op1=ALU.add,
-            )
-        tanh2_of = {}
-        for e in range(MEMBERS):
-            tanh2_of[e] = tail.tile(member_shape, F32, name="tanh2_%d" % e, tag="tanh2", bufs=MEMBERS)
-            nc.scalar.activation(out=tanh2_of[e][:], in_=size2_of[e][:], func=ACT.Tanh, scale=0.5)
-        for e in range(MEMBERS):
-            log2 = tail.tile(member_shape, F32, name="log2_%d" % e, tag="log2")
-            nc.scalar.activation(out=log2[:], in_=tanh2_of[e][:], func=ACT.Ln, scale=0.5, bias=half[:])
-            logvar = tail.tile(member_shape, F32, name="logvar_%d" % e, tag="logvar")
-            nc.vector.tensor_tensor(out=logvar[:], in0=floor_of[e][:], in1=log2[:], op=ALU.subtract)
-            nc.sync.dma_start(
-                out=out_1[e].rearrange("(p j) o -> p (j o)", j=UNITS),
-                in_=logvar[:].rearrange("p j o -> p (j o)"),
-            )
+            for m in range(MEMBERS - 1):
+                finish_bounds(m)
+            take_logs(MEMBERS - 1)
+            finish_bounds(MEMBERS - 1)

@@ -24,9 +24,10 @@ K_PASS = P * PACK
 PASSES = HIDDEN // K_PASS
 BANK = 512
 UNITS = BATCH // P
-CHUNKS = ((0, 512), (512, 768), (768, 896))
+HALVES = ((0, BANK), (BANK, BATCH))
+CHUNKS = (((0, 512),), ((512, 768), (768, 896)))
+N_HALVES = MEMBERS * len(HALVES)
 PLANES_PER_TILE = 4
-HEAD_GROUPS = ((0, 4), (4, 7))
 STEPS = 4
 UNITS_PER_STEP = 2
 
@@ -38,10 +39,13 @@ def tile_ensembledynamicsmodel_pa_t_e_kernel(
 ):
     nc = tc.nc
     member_shape = [P, UNITS, OUT]
-    with ExitStack() as whole:
-        keep = whole.enter_context(tc.tile_pool(name="keep", bufs=1))
-        bounds = whole.enter_context(tc.tile_pool(name="bounds", bufs=MEMBERS))
-        whole.enter_context(tc.manual_schedule())
+    with ExitStack() as ctx:
+        keep = ctx.enter_context(tc.tile_pool(name="keep", bufs=1))
+        bounds = ctx.enter_context(tc.tile_pool(name="bounds", bufs=MEMBERS))
+        loads = ctx.enter_context(tc.tile_pool(name="loads", bufs=3))
+        work = ctx.enter_context(tc.tile_pool(name="work", bufs=2))
+        psum = ctx.enter_context(tc.psum_pool(name="psum", bufs=2))
+        ctx.enter_context(tc.manual_schedule())
 
         ident = keep.tile([P, P], F32)
         make_identity(nc, ident[:])
@@ -71,217 +75,201 @@ def tile_ensembledynamicsmodel_pa_t_e_kernel(
         shift = keep.tile([P, MEMBERS, OUT2], F32)
         span = keep.tile([P, OUT], F32)
 
+        h2_of = {}
+        w3_raw_of = {}
+        w3_of = {}
+        turned_of = {}
+        grouped_of = {}
+        codes_of = {}
+        sums_of = {}
+        rows_of = {}
+        folded_of = {}
+        head_of = {}
+        results_of = {}
+        c_of = {}
+        tanh_of = {}
         product_of = {}
         abs_tau_of = {}
         floor_of = {}
 
-        with ExitStack() as main:
-            loads = main.enter_context(tc.tile_pool(name="loads", bufs=2))
-            work = main.enter_context(tc.tile_pool(name="work", bufs=2))
-            psum = main.enter_context(tc.psum_pool(name="psum", bufs=2))
+        def width_of(q):
+            return HALVES[q % 2][1] - HALVES[q % 2][0]
 
-            h2_of = {}
-            w3_raw_of = {}
-            w3_of = {}
-            grouped_a_of = {}
-            turned_of = {}
-            codes_a_of = {}
-            sums_of = {}
-            rows_of = {}
-            folded_of = {}
-            grouped_c_of = {}
-            codes_c_of = {}
-            head_of = {}
-            results_of = {}
+        def units_of(q):
+            return range(HALVES[q % 2][0] // P, HALVES[q % 2][1] // P)
 
-            def load_h2(m, units):
-                if units[0] == 0:
-                    h2_of[m] = loads.tile([P, UNITS, HIDDEN], BF16, name="h2_%d" % m, tag="h2")
-                rows = h2[m].rearrange("(p j) k -> p j k", j=UNITS)
-                for j in units:
-                    nc.sync.dma_start(out=h2_of[m][:, j, :], in_=rows[:, j, :])
+        def load_h2(q):
+            units = units_of(q)
+            h2_of[q] = loads.tile([P, len(units), HIDDEN], BF16, name="h2_%d" % q, tag="h2")
+            rows = h2[q // 2].rearrange("(p j) k -> p j k", j=UNITS)
+            for first in range(0, len(units), UNITS_PER_STEP):
+                last = min(first + UNITS_PER_STEP, len(units))
+                nc.sync.dma_start(out=h2_of[q][:, first:last, :], in_=rows[:, units[0] + first : units[0] + last, :])
 
-            def load_w3_half(m, h):
-                for g in range(PASSES):
-                    words = w3_words[PASSES * m + g].rearrange("p n t -> p (n t)")
-                    nc.sync.dma_start(
-                        out=w3_raw_of[m][:, g, h * K_PASS : (h + 1) * K_PASS].bitcast(I32),
-                        in_=words[:, h * K_PASS * PACK : (h + 1) * K_PASS * PACK].bitcast(I32),
-                    )
-
-            def load_w3_planes(a):
-                first = a * PLANES_PER_TILE
-                n_planes = min(PLANES_PER_TILE, n_passes - first)
-                for quadrant in range(4):
-                    nc.sync.dma_start(
-                        out=w3_planes_raw[32 * quadrant : 32 * quadrant + 4 * n_planes, a, :].bitcast(I32),
-                        in_=w3_scales[first : first + n_planes, 4 * quadrant : 4 * quadrant + 4, :].bitcast(I32),
-                    )
-
-            def new_w3_raw(m):
+        def load_w3_half(m, h):
+            if h == 0:
                 w3_raw_of[m] = loads.tile([P, PASSES, HIDDEN], U32, name="w3_raw_%d" % m, tag="w3_raw", bufs=1)
-
-            new_w3_raw(0)
-            load_w3_half(0, 0)
-            load_w3_planes(0)
-            load_h2(0, range(0, CHUNKS[0][1] // P))
-            load_w3_half(0, 1)
-            load_h2(0, range(CHUNKS[0][1] // P, UNITS))
-            b3_view = b3.rearrange("e o (h r s t) -> s (e o h) r t", h=PASSES, s=STEPS, t=PACK)
-            for s in range(STEPS):
+            for g in range(PASSES):
+                words = w3_words[PASSES * m + g].rearrange("p n t -> p (n t)")
                 nc.sync.dma_start(
-                    out=b3_rows[s : MEMBERS * PASSES * STEPS : STEPS, :].rearrange("c (r t) -> c r t", t=PACK),
-                    in_=b3_view[s],
+                    out=w3_raw_of[m][:, g, h * K_PASS : (h + 1) * K_PASS].bitcast(I32),
+                    in_=words[:, h * K_PASS * PACK : (h + 1) * K_PASS * PACK].bitcast(I32),
                 )
-            for a in range(1, n_plane_tiles):
-                load_w3_planes(a)
+
+        def load_w3_planes(a):
+            first = a * PLANES_PER_TILE
+            n_planes = min(PLANES_PER_TILE, n_passes - first)
             for quadrant in range(4):
                 nc.sync.dma_start(
-                    out=w4_planes[32 * quadrant : 32 * quadrant + 4, :, :].bitcast(I32),
-                    in_=w4_scales[:, 4 * quadrant : 4 * quadrant + 4, :].rearrange("c r n -> r c n").bitcast(I32),
+                    out=w3_planes_raw[32 * quadrant : 32 * quadrant + 4 * n_planes, a, :].bitcast(I32),
+                    in_=w3_scales[first : first + n_planes, 4 * quadrant : 4 * quadrant + 4, :].bitcast(I32),
                 )
+
+        load_w3_half(0, 0)
+        load_w3_planes(0)
+        load_h2(0)
+        load_w3_half(0, 1)
+        b3_view = b3.rearrange("e o (h r s t) -> s (e o h) r t", h=PASSES, s=STEPS, t=PACK)
+        for s in range(STEPS):
             nc.sync.dma_start(
-                out=w4_codes[:].bitcast(I32),
-                in_=w4_words.rearrange("c p n t -> p c (n t)").bitcast(I32),
+                out=b3_rows[s : MEMBERS * PASSES * STEPS : STEPS, :].rearrange("c (r t) -> c r t", t=PACK),
+                in_=b3_view[s],
             )
+        load_h2(1)
+        for a in range(1, n_plane_tiles):
+            load_w3_planes(a)
+        for quadrant in range(4):
             nc.sync.dma_start(
-                out=b4_all[:].rearrange("p e n -> p (e n)"),
-                in_=b4.rearrange("e o n -> (e o n)").partition_broadcast(P),
+                out=w4_planes[32 * quadrant : 32 * quadrant + 4, :, :].bitcast(I32),
+                in_=w4_scales[:, 4 * quadrant : 4 * quadrant + 4, :].rearrange("c r n -> r c n").bitcast(I32),
             )
-            nc.sync.dma_start(out=max_lv[:], in_=max_logvar[0, :].partition_broadcast(P))
-            nc.sync.dma_start(out=min_lv[:], in_=min_logvar[0, :].partition_broadcast(P))
+        nc.sync.dma_start(
+            out=w4_codes[:].bitcast(I32),
+            in_=w4_words.rearrange("c p n t -> p c (n t)").bitcast(I32),
+        )
+        nc.sync.dma_start(
+            out=b4_all[:].rearrange("p e n -> p (e n)"),
+            in_=b4.rearrange("e o n -> (e o n)").partition_broadcast(P),
+        )
+        nc.sync.dma_start(out=max_lv[:], in_=max_logvar[0, :].partition_broadcast(P))
+        nc.sync.dma_start(out=min_lv[:], in_=min_logvar[0, :].partition_broadcast(P))
 
-            def sort_w3(m, h):
-                if h == 0:
-                    w3_of[m] = work.tile([P, PASSES, HIDDEN], U32, name="w3_%d" % m, tag="w3", align_bytes=64)
-                cols = slice(h * K_PASS, (h + 1) * K_PASS)
-                if (PASSES * m) % PLANES_PER_TILE == 0:
-                    a = (PASSES * m) // PLANES_PER_TILE
-                    nc.vector.tensor_copy(
-                        out=w3_planes[:, a, cols].bitcast(I32).rearrange("p (s r) -> p s r", s=STEPS),
-                        in_=w3_planes_raw[:, a, cols].bitcast(I32).rearrange("p (r s) -> p s r", s=STEPS),
-                    )
-                for g in range(PASSES):
-                    nc.vector.tensor_copy(
-                        out=w3_of[m][:, g, cols].bitcast(I32).rearrange("p (s r t) -> p s r t", s=STEPS, t=PACK),
-                        in_=w3_raw_of[m][:, g, cols].bitcast(I32).rearrange("p (r s t) -> p s r t", s=STEPS, t=PACK),
-                    )
-
-            def chunk_of_unit(j):
-                return [i for i in range(len(CHUNKS)) if CHUNKS[i][0] <= j * P < CHUNKS[i][1]][0]
-
-            def code_column(i, g):
-                first, last = CHUNKS[i]
-                return PASSES * first + g * (last - first)
-
-            def transpose_h2(m, j):
-                words = h2_of[m][:, j, :].bitcast(F32)
-                bank = psum.tile([P, PASSES * 2, P], F32, name="turned_%d_%d" % (m, j), tag="turned")
-                for g in range(PASSES):
-                    for u in range(2):
-                        nc.tensor.transpose(
-                            out=bank[:, 2 * g + u, :],
-                            in_=words[:, 256 * g + u : 256 * (g + 1) : 2],
-                            identity=ident[:],
-                        )
-                turned_of[(m, j)] = bank
-
-            def copy_out_h2(m, j):
-                i = chunk_of_unit(j)
-                first, last = CHUNKS[i]
-                if j * P == first:
-                    grouped_a_of[(m, i)] = work.tile(
-                        [P, PASSES, last - first, PACK], BF16, name="grouped_a_%d_%d" % (m, i), tag="grouped_a", align_bytes=64
-                    )
-                nc.scalar.copy(
-                    out=grouped_a_of[(m, i)][:, :, j * P - first : (j + 1) * P - first, :].bitcast(F32),
-                    in_=turned_of[(m, j)][:].rearrange("p (g u) r -> p g r u", u=2),
+        def sort_w3(m, h):
+            if h == 0:
+                w3_of[m] = work.tile([P, PASSES, HIDDEN], U32, name="w3_%d" % m, tag="w3", align_bytes=64)
+            cols = slice(h * K_PASS, (h + 1) * K_PASS)
+            if (PASSES * m) % PLANES_PER_TILE == 0:
+                a = (PASSES * m) // PLANES_PER_TILE
+                nc.vector.tensor_copy(
+                    out=w3_planes[:, a, cols].bitcast(I32).rearrange("p (s r) -> p s r", s=STEPS),
+                    in_=w3_planes_raw[:, a, cols].bitcast(I32).rearrange("p (r s) -> p s r", s=STEPS),
+                )
+            for g in range(PASSES):
+                nc.vector.tensor_copy(
+                    out=w3_of[m][:, g, cols].bitcast(I32).rearrange("p (s r t) -> p s r t", s=STEPS, t=PACK),
+                    in_=w3_raw_of[m][:, g, cols].bitcast(I32).rearrange("p (r s t) -> p s r t", s=STEPS, t=PACK),
                 )
 
-            def quantise_h2(m, i):
-                first, last = CHUNKS[i]
-                if i == 0:
-                    codes = work.tile([P, PASSES * BATCH], U32, name="codes_a_%d" % m, tag="codes_a", align_bytes=64)
-                    plane = work.tile([P, PASSES * BATCH], U8, name="plane_a_%d" % m, tag="plane_a", align_bytes=64)
-                    codes_a_of[m] = (codes, plane)
-                codes, plane = codes_a_of[m]
+        def code_column(q, first, last, g):
+            return PASSES * (first - HALVES[q % 2][0]) + g * (last - first)
+
+        def new_grouped(stage, q):
+            for first, last in CHUNKS[q % 2]:
+                grouped_of[(stage, q, first)] = work.tile(
+                    [P, PASSES, last - first, PACK], BF16, name="grouped_%s_%d_%d" % (stage, q, first),
+                    tag="grouped_%s_%d" % (stage, first), bufs=1, align_bytes=64,
+                )
+
+        def quantise(stage, q):
+            codes = work.tile([P, PASSES * width_of(q)], U32, name="codes_%s_%d" % (stage, q), tag="codes_" + stage, bufs=3, align_bytes=64)
+            plane = work.tile([P, PASSES * width_of(q)], U8, name="plane_%s_%d" % (stage, q), tag="plane_" + stage, bufs=3, align_bytes=64)
+            codes_of[(stage, q)] = (codes, plane)
+            for first, last in CHUNKS[q % 2]:
+                cols = slice(code_column(q, first, last, 0), code_column(q, first, last, PASSES))
                 nc.vector.quantize_mx(
-                    out=codes[:, PASSES * first : PASSES * last].bitcast(FP8X4),
-                    scales=plane[:, PASSES * first : PASSES * last],
-                    in_=grouped_a_of[(m, i)][:].rearrange("p g r t -> p (g r t)"),
+                    out=codes[:, cols].bitcast(FP8X4),
+                    scales=plane[:, cols],
+                    in_=grouped_of[(stage, q, first)][:].rearrange("p g r t -> p (g r t)"),
                 )
 
-            def first_matmul(m, s, h):
-                codes, plane = codes_a_of[m]
-                tile_cols = slice((h * STEPS + s) * P, (h * STEPS + s + 1) * P)
-                wide = psum.tile([P, BANK], F32, name="wide_%d_%d_%d" % (m, s, h), tag="wide")
-                narrow = psum.tile([P, BATCH - BANK], F32, name="narrow_%d_%d_%d" % (m, s, h), tag="narrow")
-                for i in range(len(CHUNKS)):
-                    first, last = CHUNKS[i]
-                    sums = wide[:] if first == 0 else narrow[:, first - BANK : last - BANK]
-                    for g in range(PASSES):
-                        c = PASSES * m + g
-                        cols = slice(code_column(i, g), code_column(i, g) + last - first)
-                        nc.tensor.matmul_mx(
-                            out=sums,
-                            lhsT=w3_of[m][:, g, tile_cols].bitcast(FP8X4),
-                            lhsT_scale=w3_planes[4 * (c % PLANES_PER_TILE) : P, c // PLANES_PER_TILE, tile_cols],
-                            rhs=codes[:, cols].bitcast(FP8X4),
-                            rhs_scale=plane[:, cols],
-                            start=(g == 0),
-                            stop=(g == PASSES - 1),
-                        )
-                sums_of[(m, s, h)] = (wide, narrow)
+        def transpose_h2(q, j):
+            words = h2_of[q][:, j - units_of(q)[0], :].bitcast(F32)
+            bank = psum.tile([P, PASSES * 2, P], F32, name="turned_%d_%d" % (q, j), tag="turned")
+            for g in range(PASSES):
+                for u in range(2):
+                    nc.tensor.transpose(
+                        out=bank[:, 2 * g + u, :],
+                        in_=words[:, 256 * g + u : 256 * (g + 1) : 2],
+                        identity=ident[:],
+                    )
+            turned_of[(q, j)] = bank
 
-            def silu(m, s, h):
-                if h == 0:
-                    rows_of[(m, s)] = work.tile([P, PASSES, BATCH], BF16, name="rows_%d_%d" % (m, s), tag="rows", bufs=4)
-                wide, narrow = sums_of[(m, s, h)]
-                column = (m * PASSES + h) * STEPS + s
-                bias = b3_columns[:, column : column + 1]
-                nc.scalar.activation(out=rows_of[(m, s)][:, h, 0:BANK], in_=wide[:], func=ACT.Silu, bias=bias)
-                nc.scalar.activation(out=rows_of[(m, s)][:, h, BANK:BATCH], in_=narrow[:], func=ACT.Silu, bias=bias)
-
-            def fold(m, s):
-                if s == 0:
-                    folded_of[m] = work.tile([P, PASSES, PACK, BATCH], BF16, name="folded_%d" % m, tag="folded")
-                for t in range(PACK):
-                    nc.sync.dma_start(out=folded_of[m][s:P:STEPS, :, t, :], in_=rows_of[(m, s)][t:P:PACK, :, :])
-
-            def regroup_h3(m, i):
-                first, last = CHUNKS[i]
-                grouped_c_of[(m, i)] = work.tile(
-                    [P, PASSES, last - first, PACK], BF16, name="grouped_c_%d_%d" % (m, i), tag="grouped_c", align_bytes=64
-                )
-                for g in range(PASSES):
-                    nc.vector.tensor_copy(
-                        out=grouped_c_of[(m, i)][:, g, :, :].rearrange("p (c i) t -> p c t i", i=4),
-                        in_=folded_of[m][:, g, :, first:last].rearrange("p t (c i) -> p c t i", i=4),
+        def copy_out_h2(q, j):
+            for first, last in CHUNKS[q % 2]:
+                if first <= j * P < last:
+                    nc.scalar.copy(
+                        out=grouped_of[("a", q, first)][:, :, j * P - first : (j + 1) * P - first, :].bitcast(F32),
+                        in_=turned_of[(q, j)][:].rearrange("p (g u) r -> p g r u", u=2),
                     )
 
-            def quantise_h3(m, i):
-                first, last = CHUNKS[i]
-                if i == 0:
-                    codes = work.tile([P, PASSES * BATCH], U32, name="codes_c_%d" % m, tag="codes_c", bufs=1, align_bytes=64)
-                    plane = work.tile([P, PASSES * BATCH], U8, name="plane_c_%d" % m, tag="plane_c", bufs=1, align_bytes=64)
-                    codes_c_of[m] = (codes, plane)
-                codes, plane = codes_c_of[m]
-                nc.vector.quantize_mx(
-                    out=codes[:, PASSES * first : PASSES * last].bitcast(FP8X4),
-                    scales=plane[:, PASSES * first : PASSES * last],
-                    in_=grouped_c_of[(m, i)][:].rearrange("p g r t -> p (g r t)"),
-                )
+        def first_matmul(q, s, h):
+            m = q // 2
+            codes, plane = codes_of[("a", q)]
+            tile_cols = slice((h * STEPS + s) * P, (h * STEPS + s + 1) * P)
+            sums = psum.tile([P, BANK], F32, name="sums_%d_%d_%d" % (q, s, h), tag="sums", bufs=4)
+            for first, last in CHUNKS[q % 2]:
+                for g in range(PASSES):
+                    c = PASSES * m + g
+                    cols = slice(code_column(q, first, last, g), code_column(q, first, last, g + 1))
+                    nc.tensor.matmul_mx(
+                        out=sums[:, first - HALVES[q % 2][0] : last - HALVES[q % 2][0]],
+                        lhsT=w3_of[m][:, g, tile_cols].bitcast(FP8X4),
+                        lhsT_scale=w3_planes[4 * (c % PLANES_PER_TILE) : P, c // PLANES_PER_TILE, tile_cols],
+                        rhs=codes[:, cols].bitcast(FP8X4),
+                        rhs_scale=plane[:, cols],
+                        start=(g == 0),
+                        stop=(g == PASSES - 1),
+                    )
+            sums_of[(q, s, h)] = sums
 
-            def second_matmul(m, group):
-                codes, plane = codes_c_of[m]
-                first, last = HEAD_GROUPS[group]
-                head_of[m] = psum.tile([P, BANK // OUT2, OUT2], F32, name="head_%d_%d" % (m, group), tag="head")
-                for j in range(first, last):
-                    i = chunk_of_unit(j)
+        def silu(q, s, h):
+            if h == 0:
+                rows_of[(q, s)] = work.tile([P, PASSES, width_of(q)], BF16, name="rows_%d_%d" % (q, s), tag="rows", bufs=6)
+            column = ((q // 2) * PASSES + h) * STEPS + s
+            nc.scalar.activation(
+                out=rows_of[(q, s)][:, h, :],
+                in_=sums_of[(q, s, h)][:, 0 : width_of(q)],
+                func=ACT.Silu,
+                bias=b3_columns[:, column : column + 1],
+            )
+
+        def fold(q, s):
+            if s == 0:
+                folded_of[q] = work.tile([P, PASSES, PACK, width_of(q)], BF16, name="folded_%d" % q, tag="folded", bufs=3)
+            for t in range(PACK):
+                nc.sync.dma_start(out=folded_of[q][s:P:STEPS, :, t, :], in_=rows_of[(q, s)][t:P:PACK, :, :])
+
+        def regroup_h3(q):
+            new_grouped("c", q)
+            for first, last in CHUNKS[q % 2]:
+                for g in range(PASSES):
+                    nc.vector.tensor_copy(
+                        out=grouped_of[("c", q, first)][:, g, :, :].rearrange("p (c i) t -> p c t i", i=4),
+                        in_=folded_of[q][:, g, :, first - HALVES[q % 2][0] : last - HALVES[q % 2][0]].rearrange(
+                            "p t (c i) -> p c t i", i=4
+                        ),
+                    )
+
+        def second_matmul(q):
+            m = q // 2
+            codes, plane = codes_of[("c", q)]
+            head_of[q] = psum.tile([P, BANK // OUT2, OUT2], F32, name="head_%d" % q, tag="head")
+            for first, last in CHUNKS[q % 2]:
+                for j in range(first // P, last // P):
                     for g in range(PASSES):
-                        start = code_column(i, g) + j * P - CHUNKS[i][0]
+                        start = code_column(q, first, last, g) + j * P - first
                         nc.tensor.matmul_mx(
-                            out=head_of[m][:, j - first, :],
+                            out=head_of[q][:, j - units_of(q)[0], :],
                             lhsT=codes[:, start : start + P].bitcast(FP8X4),
                             lhsT_scale=plane[:, start : start + P],
                             rhs=w4_codes[:, PASSES * m + g, :].bitcast(FP8X4),
@@ -290,138 +278,153 @@ def tile_ensembledynamicsmodel_pa_t_e_kernel(
                             stop=(g == PASSES - 1),
                         )
 
-            def add_b4(m, group):
-                first, last = HEAD_GROUPS[group]
-                if group == 0:
-                    results_of[m] = work.tile([P, 2, UNITS, OUT], F32, name="results_%d" % m, tag="results")
-                nc.vector.tensor_tensor(
-                    out=results_of[m][:, :, first:last, :].rearrange("p h j o -> p j h o"),
-                    in0=head_of[m][:, 0 : last - first, :].rearrange("p j (h o) -> p j h o", h=2),
-                    in1=shift[:, m, :].rearrange("p (h o) -> p h o", h=2).unsqueeze(1).to_broadcast([P, last - first, 2, OUT]),
-                    op=ALU.add,
-                )
+        def add_b4(q):
+            m = q // 2
+            units = units_of(q)
+            if q % 2 == 0:
+                results_of[m] = work.tile([P, 2, UNITS, OUT], F32, name="results_%d" % m, tag="results")
+            nc.vector.tensor_tensor(
+                out=results_of[m][:, :, units[0] : units[0] + len(units), :].rearrange("p h j o -> p j h o"),
+                in0=head_of[q][:, 0 : len(units), :].rearrange("p j (h o) -> p j h o", h=2),
+                in1=shift[:, m, :].rearrange("p (h o) -> p h o", h=2).unsqueeze(1).to_broadcast([P, len(units), 2, OUT]),
+                op=ALU.add,
+            )
 
-            def begin_bounds(m):
-                nc.sync.dma_start(
-                    out=out_0[m].rearrange("(p j) o -> p (j o)", j=UNITS),
-                    in_=results_of[m][:, 0, :, :].rearrange("p j o -> p (j o)"),
-                )
-                u = results_of[m][:, 1, :, :]
-                minus_size = work.tile(member_shape, F32, name="minus_size_%d" % m, tag="minus_size")
-                nc.vector.scalar_tensor_tensor(out=minus_size[:], in0=u, scalar=-1.0, in1=u, op0=ALU.mult, op1=ALU.min)
-                c = work.tile(member_shape, F32, name="c_%d" % m, tag="c")
-                nc.vector.scalar_tensor_tensor(
-                    out=c[:],
-                    in0=u,
-                    scalar=0.0,
-                    in1=span[:].unsqueeze(1).to_broadcast(member_shape),
-                    op0=ALU.min,
-                    op1=ALU.add,
-                )
-                eta = work.tile(member_shape, F32, name="eta_%d" % m, tag="eta")
-                nc.scalar.activation(out=eta[:], in_=minus_size[:], func=ACT.Tanh, scale=0.5)
-                tau = work.tile(member_shape, F32, name="tau_%d" % m, tag="tau")
-                nc.scalar.activation(out=tau[:], in_=c[:], func=ACT.Tanh, scale=0.5)
-                floor_of[m] = bounds.tile(member_shape, F32, name="floor_%d" % m, tag="floor")
-                nc.vector.scalar_tensor_tensor(
-                    out=floor_of[m][:],
-                    in0=c[:],
-                    scalar=0.0,
-                    in1=min_lv[:].unsqueeze(1).to_broadcast(member_shape),
-                    op0=ALU.max,
-                    op1=ALU.add,
-                )
-                one_plus_eta = work.tile(member_shape, F32, name="one_plus_eta_%d" % m, tag="one_plus_eta")
-                nc.vector.tensor_scalar_add(out=one_plus_eta[:], in0=eta[:], scalar1=1.0)
-                product_of[m] = bounds.tile(member_shape, F32, name="product_%d" % m, tag="product")
-                nc.vector.scalar_tensor_tensor(
-                    out=product_of[m][:], in0=tau[:], scalar=1.0, in1=one_plus_eta[:], op0=ALU.add, op1=ALU.mult
-                )
-                abs_tau_of[m] = bounds.tile(member_shape, F32, name="abs_tau_%d" % m, tag="abs_tau")
-                nc.vector.scalar_tensor_tensor(
-                    out=abs_tau_of[m][:], in0=tau[:], scalar=-1.0, in1=tau[:], op0=ALU.mult, op1=ALU.max
-                )
+        def bounds_inputs(m):
+            nc.sync.dma_start(
+                out=out_0[m].rearrange("(p j) o -> p (j o)", j=UNITS),
+                in_=results_of[m][:, 0, :, :].rearrange("p j o -> p (j o)"),
+            )
+            u = results_of[m][:, 1, :, :]
+            minus_size = work.tile(member_shape, F32, name="minus_size_%d" % m, tag="minus_size")
+            nc.vector.scalar_tensor_tensor(out=minus_size[:], in0=u, scalar=-1.0, in1=u, op0=ALU.mult, op1=ALU.min)
+            c = work.tile(member_shape, F32, name="c_%d" % m, tag="c")
+            nc.vector.scalar_tensor_tensor(
+                out=c[:],
+                in0=u,
+                scalar=0.0,
+                in1=span[:].unsqueeze(1).to_broadcast(member_shape),
+                op0=ALU.min,
+                op1=ALU.add,
+            )
+            floor_of[m] = bounds.tile(member_shape, F32, name="floor_%d" % m, tag="floor")
+            nc.vector.scalar_tensor_tensor(
+                out=floor_of[m][:],
+                in0=c[:],
+                scalar=0.0,
+                in1=min_lv[:].unsqueeze(1).to_broadcast(member_shape),
+                op0=ALU.max,
+                op1=ALU.add,
+            )
+            c_of[m] = (minus_size, c)
 
-            def take_logs(m):
-                nc.scalar.activation(out=product_of[m][:], in_=product_of[m][:], func=ACT.Ln, scale=-0.5, bias=two[:])
-                nc.scalar.activation(out=abs_tau_of[m][:], in_=abs_tau_of[m][:], func=ACT.Ln, bias=one[:])
+        def bounds_tanh(m):
+            minus_size, c = c_of[m]
+            eta = work.tile(member_shape, F32, name="eta_%d" % m, tag="eta")
+            nc.scalar.activation(out=eta[:], in_=minus_size[:], func=ACT.Tanh, scale=0.5)
+            tau = work.tile(member_shape, F32, name="tau_%d" % m, tag="tau")
+            nc.scalar.activation(out=tau[:], in_=c[:], func=ACT.Tanh, scale=0.5)
+            one_plus_eta = work.tile(member_shape, F32, name="one_plus_eta_%d" % m, tag="one_plus_eta")
+            nc.scalar.activation(out=one_plus_eta[:], in_=eta[:], func=ACT.Identity, bias=one[:])
+            abs_tau_of[m] = bounds.tile(member_shape, F32, name="abs_tau_%d" % m, tag="abs_tau")
+            nc.scalar.activation(out=abs_tau_of[m][:], in_=tau[:], func=ACT.Abs)
+            tanh_of[m] = (one_plus_eta, tau)
 
-            def finish_bounds(m):
-                nc.vector.tensor_tensor(out=floor_of[m][:], in0=floor_of[m][:], in1=product_of[m][:], op=ALU.add)
-                nc.vector.tensor_tensor(out=floor_of[m][:], in0=floor_of[m][:], in1=abs_tau_of[m][:], op=ALU.subtract)
-                nc.sync.dma_start(
-                    out=out_1[m].rearrange("(p j) o -> p (j o)", j=UNITS),
-                    in_=floor_of[m][:].rearrange("p j o -> p (j o)"),
-                )
+        def bounds_product(m):
+            one_plus_eta, tau = tanh_of[m]
+            product_of[m] = bounds.tile(member_shape, F32, name="product_%d" % m, tag="product")
+            nc.vector.scalar_tensor_tensor(
+                out=product_of[m][:], in0=tau[:], scalar=1.0, in1=one_plus_eta[:], op0=ALU.add, op1=ALU.mult
+            )
 
-            for e in range(-1, MEMBERS + 1):
-                ahead = e + 1
-                behind = e - 1
-                does_a = ahead < MEMBERS
-                does_b = 0 <= e < MEMBERS
-                does_cd = 0 <= behind
-                for s in range(STEPS):
-                    units = range(s * UNITS_PER_STEP, min((s + 1) * UNITS_PER_STEP, UNITS))
-                    if s == 0 and e + 2 < MEMBERS:
-                        load_h2(e + 2, range(UNITS))
-                    if s == 2 and e + 2 < MEMBERS:
-                        new_w3_raw(e + 2)
-                        for h in range(PASSES):
-                            load_w3_half(e + 2, h)
+        def take_logs(m):
+            nc.scalar.activation(out=product_of[m][:], in_=product_of[m][:], func=ACT.Ln, scale=-0.5, bias=two[:])
+            nc.scalar.activation(out=abs_tau_of[m][:], in_=abs_tau_of[m][:], func=ACT.Ln, bias=one[:])
 
-                    if does_a:
-                        for j in units:
-                            transpose_h2(ahead, j)
-                    if e == -1 and s == STEPS - 1:
-                        nc.vector.tensor_copy(out=b3_rows_f32[:], in_=b3_rows[:])
-                        b3_turned = psum.tile([P, PASSES * 2, P], F32, name="b3_turned", tag="turned")
-                        nc.tensor.transpose(out=b3_turned[:, 0, :], in_=b3_rows_f32[:], identity=ident[:])
-                    if does_b:
-                        for h in range(PASSES):
-                            first_matmul(e, s, h)
-                    if does_cd and s >= STEPS - len(HEAD_GROUPS):
-                        second_matmul(behind, s - (STEPS - len(HEAD_GROUPS)))
+        def finish_bounds(m):
+            nc.vector.tensor_tensor(out=floor_of[m][:], in0=floor_of[m][:], in1=product_of[m][:], op=ALU.add)
+            nc.vector.tensor_tensor(out=floor_of[m][:], in0=floor_of[m][:], in1=abs_tau_of[m][:], op=ALU.subtract)
+            nc.sync.dma_start(
+                out=out_1[m].rearrange("(p j) o -> p (j o)", j=UNITS),
+                in_=floor_of[m][:].rearrange("p j o -> p (j o)"),
+            )
 
-                    if does_a:
-                        for j in units:
-                            copy_out_h2(ahead, j)
-                    if does_b:
-                        for h in range(PASSES):
-                            silu(e, s, h)
-                        fold(e, s)
-                    if e == MEMBERS and s == 0:
-                        for m in range(MEMBERS - 1):
-                            take_logs(m)
+        for q in range(-2, N_HALVES + 2):
+            does_a = 0 <= q + 1 < N_HALVES
+            does_b = 0 <= q < N_HALVES
+            does_c = 0 <= q - 1 < N_HALVES
+            does_d = 0 <= q - 2 < N_HALVES
+            next_member = q // 2 + 1
+            done_member = (q - 2) // 2
+            for s in range(STEPS):
+                units = []
+                if does_a:
+                    units = list(units_of(q + 1))[s * UNITS_PER_STEP : (s + 1) * UNITS_PER_STEP]
+                if s == 0 and 2 <= q + 3 < N_HALVES:
+                    load_h2(q + 3)
+                if s == 2 and q % 2 == 1 and next_member + 1 < MEMBERS:
+                    for h in range(PASSES):
+                        load_w3_half(next_member + 1, h)
 
-                    if e == -1 and s == STEPS - 1:
-                        nc.vector.tensor_copy(out=b3_columns[:], in_=b3_turned[:, 0, 0 : MEMBERS * PASSES * STEPS])
-                    if e == 0 and s == 0:
-                        nc.vector.tensor_copy(out=shift[:, :, 0:OUT], in_=b4_all[:, :, 0:OUT])
-                        nc.vector.tensor_tensor(
-                            out=shift[:, :, OUT:OUT2],
-                            in0=b4_all[:, :, OUT:OUT2],
-                            in1=max_lv[:].unsqueeze(1).to_broadcast([P, MEMBERS, OUT]),
-                            op=ALU.subtract,
-                        )
-                        nc.vector.tensor_tensor(out=span[:], in0=max_lv[:], in1=min_lv[:], op=ALU.subtract)
-                    if does_a and s == 0:
-                        sort_w3(ahead, 0)
-                    if does_cd and s < len(CHUNKS):
-                        regroup_h3(behind, s)
-                    if does_a:
-                        for i in range(len(CHUNKS)):
-                            if (CHUNKS[i][1] // P - 1) // UNITS_PER_STEP == s:
-                                quantise_h2(ahead, i)
-                    if does_a and s == 1:
-                        sort_w3(ahead, 1)
-                    if does_cd and s < len(CHUNKS):
-                        quantise_h3(behind, s)
-                    if does_cd and s >= STEPS - len(HEAD_GROUPS):
-                        add_b4(behind, s - (STEPS - len(HEAD_GROUPS)))
-                    if does_cd and s == STEPS - 1:
-                        begin_bounds(behind)
+                for j in units:
+                    transpose_h2(q + 1, j)
+                if q == -1 and s == STEPS - 1:
+                    nc.vector.tensor_copy(out=b3_rows_f32[:], in_=b3_rows[:])
+                    b3_turned = psum.tile([P, PASSES * 2, P], F32, name="b3_turned", tag="turned")
+                    nc.tensor.transpose(out=b3_turned[:, 0, :], in_=b3_rows_f32[:], identity=ident[:])
+                if does_d and s == 0:
+                    second_matmul(q - 2)
+                if does_b:
+                    for h in range(PASSES):
+                        first_matmul(q, s, h)
 
-            for m in range(MEMBERS - 1):
-                finish_bounds(m)
-            take_logs(MEMBERS - 1)
-            finish_bounds(MEMBERS - 1)
+                if does_a and s == 0:
+                    new_grouped("a", q + 1)
+                for j in units:
+                    copy_out_h2(q + 1, j)
+                if does_b:
+                    for h in range(PASSES):
+                        silu(q, s, h)
+                    fold(q, s)
+                if q % 2 == 1 and s == 1 and 0 <= done_member < MEMBERS - 1:
+                    bounds_tanh(done_member)
+
+                if q == -1 and s == STEPS - 1:
+                    nc.vector.tensor_copy(out=b3_columns[:], in_=b3_turned[:, 0, 0 : MEMBERS * PASSES * STEPS])
+                if q == 0 and s == 0:
+                    nc.vector.tensor_copy(out=shift[:, :, 0:OUT], in_=b4_all[:, :, 0:OUT])
+                    nc.vector.tensor_tensor(
+                        out=shift[:, :, OUT:OUT2],
+                        in0=b4_all[:, :, OUT:OUT2],
+                        in1=max_lv[:].unsqueeze(1).to_broadcast([P, MEMBERS, OUT]),
+                        op=ALU.subtract,
+                    )
+                    nc.vector.tensor_tensor(out=span[:], in0=max_lv[:], in1=min_lv[:], op=ALU.subtract)
+                if q % 2 == 0 and s == 0 and 0 <= done_member - 1 < MEMBERS - 1:
+                    bounds_product(done_member - 1)
+                if s == 0 and next_member < MEMBERS:
+                    sort_w3(next_member, q % 2)
+                if does_d and s == 0:
+                    add_b4(q - 2)
+                    if q % 2 == 1 and done_member < MEMBERS - 1:
+                        bounds_inputs(done_member)
+                if does_c and s == 1:
+                    regroup_h3(q - 1)
+                if does_a and s == 2:
+                    quantise("a", q + 1)
+                if does_c and s == 2:
+                    quantise("c", q - 1)
+                if q == N_HALVES and s == 0:
+                    for m in range(MEMBERS - 1):
+                        take_logs(m)
+
+        last_member = MEMBERS - 1
+        bounds_inputs(last_member)
+        bounds_tanh(last_member)
+        finish_bounds(0)
+        finish_bounds(1)
+        bounds_product(last_member)
+        take_logs(last_member)
+        finish_bounds(2)
+        finish_bounds(3)
+        finish_bounds(last_member)

@@ -24,10 +24,9 @@ K_PASS = P * PACK
 PASSES = HIDDEN // K_PASS
 BANK = 512
 UNITS = BATCH // P
-HALVES = ((0, BANK), (BANK, BATCH))
-CHUNKS = (((0, 512),), ((512, 768), (768, 896)))
-N_HALVES = MEMBERS * len(HALVES)
+CHUNKS = ((0, 512), (512, 768), (768, 896))
 PLANES_PER_TILE = 4
+HEAD_GROUPS = ((0, 4), (4, 7))
 STEPS = 4
 UNITS_PER_STEP = 2
 
@@ -39,13 +38,10 @@ def tile_ensembledynamicsmodel_pa_t_e_kernel(
 ):
     nc = tc.nc
     member_shape = [P, UNITS, OUT]
-    with ExitStack() as ctx:
-        keep = ctx.enter_context(tc.tile_pool(name="keep", bufs=1))
-        bounds = ctx.enter_context(tc.tile_pool(name="bounds", bufs=MEMBERS))
-        loads = ctx.enter_context(tc.tile_pool(name="loads", bufs=3))
-        work = ctx.enter_context(tc.tile_pool(name="work", bufs=2))
-        psum = ctx.enter_context(tc.psum_pool(name="psum", bufs=2))
-        ctx.enter_context(tc.manual_schedule())
+    with ExitStack() as whole:
+        keep = whole.enter_context(tc.tile_pool(name="keep", bufs=1))
+        bounds = whole.enter_context(tc.tile_pool(name="bounds", bufs=MEMBERS))
+        whole.enter_context(tc.manual_schedule())
 
         ident = keep.tile([P, P], F32)
         make_identity(nc, ident[:])
@@ -75,201 +71,218 @@ def tile_ensembledynamicsmodel_pa_t_e_kernel(
         shift = keep.tile([P, MEMBERS, OUT2], F32)
         span = keep.tile([P, OUT], F32)
 
-        h2_of = {}
-        w3_raw_of = {}
-        w3_of = {}
-        turned_of = {}
-        grouped_of = {}
-        codes_of = {}
-        sums_of = {}
-        rows_of = {}
-        folded_of = {}
-        head_of = {}
-        results_of = {}
-        c_of = {}
-        tanh_of = {}
         product_of = {}
         abs_tau_of = {}
         floor_of = {}
 
-        def width_of(q):
-            return HALVES[q % 2][1] - HALVES[q % 2][0]
+        with ExitStack() as main:
+            loads = main.enter_context(tc.tile_pool(name="loads", bufs=2))
+            work = main.enter_context(tc.tile_pool(name="work", bufs=2))
+            psum = main.enter_context(tc.psum_pool(name="psum", bufs=2))
 
-        def units_of(q):
-            return range(HALVES[q % 2][0] // P, HALVES[q % 2][1] // P)
+            h2_of = {}
+            w3_raw_of = {}
+            w3_of = {}
+            grouped_a_of = {}
+            turned_of = {}
+            codes_a_of = {}
+            sums_of = {}
+            rows_of = {}
+            folded_of = {}
+            grouped_c_of = {}
+            codes_c_of = {}
+            head_of = {}
+            results_of = {}
 
-        def load_h2(q):
-            units = units_of(q)
-            h2_of[q] = loads.tile([P, len(units), HIDDEN], BF16, name="h2_%d" % q, tag="h2")
-            rows = h2[q // 2].rearrange("(p j) k -> p j k", j=UNITS)
-            for first in range(0, len(units), UNITS_PER_STEP):
-                last = min(first + UNITS_PER_STEP, len(units))
-                nc.sync.dma_start(out=h2_of[q][:, first:last, :], in_=rows[:, units[0] + first : units[0] + last, :])
+            def load_h2(m, units):
+                if units[0] == 0:
+                    h2_of[m] = loads.tile([P, UNITS, HIDDEN], BF16, name="h2_%d" % m, tag="h2")
+                rows = h2[m].rearrange("(p j) k -> p j k", j=UNITS)
+                first, last = units[0], units[0] + len(units)
+                nc.sync.dma_start(out=h2_of[m][:, first:last, :], in_=rows[:, first:last, :])
 
-        def load_w3_half(m, h):
-            if h == 0:
-                w3_raw_of[m] = loads.tile([P, PASSES, HIDDEN], U32, name="w3_raw_%d" % m, tag="w3_raw", bufs=1)
-            for g in range(PASSES):
-                words = w3_words[PASSES * m + g].rearrange("p n t -> p (n t)")
+            def load_w3_half(m, h):
+                words = w3_words[PASSES * m : PASSES * (m + 1)].rearrange("g p n t -> p g (n t)")
                 nc.sync.dma_start(
-                    out=w3_raw_of[m][:, g, h * K_PASS : (h + 1) * K_PASS].bitcast(I32),
-                    in_=words[:, h * K_PASS * PACK : (h + 1) * K_PASS * PACK].bitcast(I32),
+                    out=w3_raw_of[m][:, :, h * K_PASS : (h + 1) * K_PASS].bitcast(I32),
+                    in_=words[:, :, h * K_PASS * PACK : (h + 1) * K_PASS * PACK].bitcast(I32),
                 )
 
-        def load_w3_planes(a):
-            first = a * PLANES_PER_TILE
-            n_planes = min(PLANES_PER_TILE, n_passes - first)
+            def load_w3_planes(a):
+                first = a * PLANES_PER_TILE
+                n_planes = min(PLANES_PER_TILE, n_passes - first)
+                for quadrant in range(4):
+                    nc.sync.dma_start(
+                        out=w3_planes_raw[32 * quadrant : 32 * quadrant + 4 * n_planes, a, :].bitcast(I32),
+                        in_=w3_scales[first : first + n_planes, 4 * quadrant : 4 * quadrant + 4, :].bitcast(I32),
+                    )
+
+            def new_w3_raw(m):
+                w3_raw_of[m] = loads.tile([P, PASSES, HIDDEN], U32, name="w3_raw_%d" % m, tag="w3_raw", bufs=1)
+
+            new_w3_raw(0)
+            load_w3_half(0, 0)
+            load_w3_planes(0)
+            load_h2(0, range(0, CHUNKS[0][1] // P))
+            load_w3_half(0, 1)
+            load_h2(0, range(CHUNKS[0][1] // P, UNITS))
+            b3_view = b3.rearrange("e o (h r s t) -> s (e o h) r t", h=PASSES, s=STEPS, t=PACK)
+            for s in range(STEPS):
+                nc.sync.dma_start(
+                    out=b3_rows[s : MEMBERS * PASSES * STEPS : STEPS, :].rearrange("c (r t) -> c r t", t=PACK),
+                    in_=b3_view[s],
+                )
+            for a in range(1, n_plane_tiles):
+                load_w3_planes(a)
             for quadrant in range(4):
                 nc.sync.dma_start(
-                    out=w3_planes_raw[32 * quadrant : 32 * quadrant + 4 * n_planes, a, :].bitcast(I32),
-                    in_=w3_scales[first : first + n_planes, 4 * quadrant : 4 * quadrant + 4, :].bitcast(I32),
+                    out=w4_planes[32 * quadrant : 32 * quadrant + 4, :, :].bitcast(I32),
+                    in_=w4_scales[:, 4 * quadrant : 4 * quadrant + 4, :].rearrange("c r n -> r c n").bitcast(I32),
                 )
-
-        load_w3_half(0, 0)
-        load_w3_planes(0)
-        load_h2(0)
-        load_w3_half(0, 1)
-        b3_view = b3.rearrange("e o (h r s t) -> s (e o h) r t", h=PASSES, s=STEPS, t=PACK)
-        for s in range(STEPS):
             nc.sync.dma_start(
-                out=b3_rows[s : MEMBERS * PASSES * STEPS : STEPS, :].rearrange("c (r t) -> c r t", t=PACK),
-                in_=b3_view[s],
+                out=w4_codes[:].bitcast(I32),
+                in_=w4_words.rearrange("c p n t -> p c (n t)").bitcast(I32),
             )
-        load_h2(1)
-        for a in range(1, n_plane_tiles):
-            load_w3_planes(a)
-        for quadrant in range(4):
             nc.sync.dma_start(
-                out=w4_planes[32 * quadrant : 32 * quadrant + 4, :, :].bitcast(I32),
-                in_=w4_scales[:, 4 * quadrant : 4 * quadrant + 4, :].rearrange("c r n -> r c n").bitcast(I32),
+                out=b4_all[:].rearrange("p e n -> p (e n)"),
+                in_=b4.rearrange("e o n -> (e o n)").partition_broadcast(P),
             )
-        nc.sync.dma_start(
-            out=w4_codes[:].bitcast(I32),
-            in_=w4_words.rearrange("c p n t -> p c (n t)").bitcast(I32),
-        )
-        nc.sync.dma_start(
-            out=b4_all[:].rearrange("p e n -> p (e n)"),
-            in_=b4.rearrange("e o n -> (e o n)").partition_broadcast(P),
-        )
-        nc.sync.dma_start(out=max_lv[:], in_=max_logvar[0, :].partition_broadcast(P))
-        nc.sync.dma_start(out=min_lv[:], in_=min_logvar[0, :].partition_broadcast(P))
+            nc.sync.dma_start(out=max_lv[:], in_=max_logvar[0, :].partition_broadcast(P))
+            nc.sync.dma_start(out=min_lv[:], in_=min_logvar[0, :].partition_broadcast(P))
 
-        def sort_w3(m, h):
-            if h == 0:
-                w3_of[m] = work.tile([P, PASSES, HIDDEN], U32, name="w3_%d" % m, tag="w3", align_bytes=64)
-            cols = slice(h * K_PASS, (h + 1) * K_PASS)
-            if (PASSES * m) % PLANES_PER_TILE == 0:
-                a = (PASSES * m) // PLANES_PER_TILE
-                nc.vector.tensor_copy(
-                    out=w3_planes[:, a, cols].bitcast(I32).rearrange("p (s r) -> p s r", s=STEPS),
-                    in_=w3_planes_raw[:, a, cols].bitcast(I32).rearrange("p (r s) -> p s r", s=STEPS),
-                )
-            for g in range(PASSES):
-                nc.vector.tensor_copy(
-                    out=w3_of[m][:, g, cols].bitcast(I32).rearrange("p (s r t) -> p s r t", s=STEPS, t=PACK),
-                    in_=w3_raw_of[m][:, g, cols].bitcast(I32).rearrange("p (r s t) -> p s r t", s=STEPS, t=PACK),
-                )
-
-        def code_column(q, first, last, g):
-            return PASSES * (first - HALVES[q % 2][0]) + g * (last - first)
-
-        def new_grouped(stage, q):
-            for first, last in CHUNKS[q % 2]:
-                grouped_of[(stage, q, first)] = work.tile(
-                    [P, PASSES, last - first, PACK], BF16, name="grouped_%s_%d_%d" % (stage, q, first),
-                    tag="grouped_%s_%d" % (stage, first), bufs=1, align_bytes=64,
-                )
-
-        def quantise(stage, q):
-            codes = work.tile([P, PASSES * width_of(q)], U32, name="codes_%s_%d" % (stage, q), tag="codes_" + stage, bufs=3, align_bytes=64)
-            plane = work.tile([P, PASSES * width_of(q)], U8, name="plane_%s_%d" % (stage, q), tag="plane_" + stage, bufs=3, align_bytes=64)
-            codes_of[(stage, q)] = (codes, plane)
-            for first, last in CHUNKS[q % 2]:
-                cols = slice(code_column(q, first, last, 0), code_column(q, first, last, PASSES))
-                nc.vector.quantize_mx(
-                    out=codes[:, cols].bitcast(FP8X4),
-                    scales=plane[:, cols],
-                    in_=grouped_of[(stage, q, first)][:].rearrange("p g r t -> p (g r t)"),
-                )
-
-        def transpose_h2(q, j):
-            words = h2_of[q][:, j - units_of(q)[0], :].bitcast(F32)
-            bank = psum.tile([P, PASSES * 2, P], F32, name="turned_%d_%d" % (q, j), tag="turned")
-            for g in range(PASSES):
-                for u in range(2):
-                    nc.tensor.transpose(
-                        out=bank[:, 2 * g + u, :],
-                        in_=words[:, 256 * g + u : 256 * (g + 1) : 2],
-                        identity=ident[:],
+            def sort_w3(m, h):
+                if h == 0:
+                    w3_of[m] = work.tile([P, PASSES, HIDDEN], U32, name="w3_%d" % m, tag="w3", align_bytes=64)
+                cols = slice(h * K_PASS, (h + 1) * K_PASS)
+                if (PASSES * m) % PLANES_PER_TILE == 0:
+                    a = (PASSES * m) // PLANES_PER_TILE
+                    nc.vector.tensor_copy(
+                        out=w3_planes[:, a, cols].bitcast(I32).rearrange("p (s r) -> p s r", s=STEPS),
+                        in_=w3_planes_raw[:, a, cols].bitcast(I32).rearrange("p (r s) -> p s r", s=STEPS),
                     )
-            turned_of[(q, j)] = bank
-
-        def copy_out_h2(q, j):
-            for first, last in CHUNKS[q % 2]:
-                if first <= j * P < last:
-                    nc.scalar.copy(
-                        out=grouped_of[("a", q, first)][:, :, j * P - first : (j + 1) * P - first, :].bitcast(F32),
-                        in_=turned_of[(q, j)][:].rearrange("p (g u) r -> p g r u", u=2),
-                    )
-
-        def first_matmul(q, s, h):
-            m = q // 2
-            codes, plane = codes_of[("a", q)]
-            tile_cols = slice((h * STEPS + s) * P, (h * STEPS + s + 1) * P)
-            sums = psum.tile([P, BANK], F32, name="sums_%d_%d_%d" % (q, s, h), tag="sums", bufs=4)
-            for first, last in CHUNKS[q % 2]:
-                for g in range(PASSES):
-                    c = PASSES * m + g
-                    cols = slice(code_column(q, first, last, g), code_column(q, first, last, g + 1))
-                    nc.tensor.matmul_mx(
-                        out=sums[:, first - HALVES[q % 2][0] : last - HALVES[q % 2][0]],
-                        lhsT=w3_of[m][:, g, tile_cols].bitcast(FP8X4),
-                        lhsT_scale=w3_planes[4 * (c % PLANES_PER_TILE) : P, c // PLANES_PER_TILE, tile_cols],
-                        rhs=codes[:, cols].bitcast(FP8X4),
-                        rhs_scale=plane[:, cols],
-                        start=(g == 0),
-                        stop=(g == PASSES - 1),
-                    )
-            sums_of[(q, s, h)] = sums
-
-        def silu(q, s, h):
-            if h == 0:
-                rows_of[(q, s)] = work.tile([P, PASSES, width_of(q)], BF16, name="rows_%d_%d" % (q, s), tag="rows", bufs=6)
-            column = ((q // 2) * PASSES + h) * STEPS + s
-            nc.scalar.activation(
-                out=rows_of[(q, s)][:, h, :],
-                in_=sums_of[(q, s, h)][:, 0 : width_of(q)],
-                func=ACT.Silu,
-                bias=b3_columns[:, column : column + 1],
-            )
-
-        def fold(q, s):
-            if s == 0:
-                folded_of[q] = work.tile([P, PASSES, PACK, width_of(q)], BF16, name="folded_%d" % q, tag="folded", bufs=3)
-            for t in range(PACK):
-                nc.sync.dma_start(out=folded_of[q][s:P:STEPS, :, t, :], in_=rows_of[(q, s)][t:P:PACK, :, :])
-
-        def regroup_h3(q):
-            new_grouped("c", q)
-            for first, last in CHUNKS[q % 2]:
                 for g in range(PASSES):
                     nc.vector.tensor_copy(
-                        out=grouped_of[("c", q, first)][:, g, :, :].rearrange("p (c i) t -> p c t i", i=4),
-                        in_=folded_of[q][:, g, :, first - HALVES[q % 2][0] : last - HALVES[q % 2][0]].rearrange(
-                            "p t (c i) -> p c t i", i=4
-                        ),
+                        out=w3_of[m][:, g, cols].bitcast(I32).rearrange("p (s r t) -> p s r t", s=STEPS, t=PACK),
+                        in_=w3_raw_of[m][:, g, cols].bitcast(I32).rearrange("p (r s t) -> p s r t", s=STEPS, t=PACK),
                     )
 
-        def second_matmul(q):
-            m = q // 2
-            codes, plane = codes_of[("c", q)]
-            head_of[q] = psum.tile([P, BANK // OUT2, OUT2], F32, name="head_%d" % q, tag="head")
-            for first, last in CHUNKS[q % 2]:
-                for j in range(first // P, last // P):
+            def chunk_of_unit(j):
+                return [i for i in range(len(CHUNKS)) if CHUNKS[i][0] <= j * P < CHUNKS[i][1]][0]
+
+            def code_column(i, g):
+                first, last = CHUNKS[i]
+                return PASSES * first + g * (last - first)
+
+            def transpose_h2(m, j):
+                words = h2_of[m][:, j, :].bitcast(F32)
+                bank = psum.tile([P, PASSES * 2, P], F32, name="turned_%d_%d" % (m, j), tag="turned")
+                for g in range(PASSES):
+                    for u in range(2):
+                        nc.tensor.transpose(
+                            out=bank[:, 2 * g + u, :],
+                            in_=words[:, 256 * g + u : 256 * (g + 1) : 2],
+                            identity=ident[:],
+                        )
+                turned_of[(m, j)] = bank
+
+            def copy_out_h2(m, j):
+                i = chunk_of_unit(j)
+                first, last = CHUNKS[i]
+                if j * P == first:
+                    grouped_a_of[(m, i)] = work.tile(
+                        [P, PASSES, last - first, PACK], BF16, name="grouped_a_%d_%d" % (m, i), tag="grouped_a", align_bytes=64
+                    )
+                nc.scalar.copy(
+                    out=grouped_a_of[(m, i)][:, :, j * P - first : (j + 1) * P - first, :].bitcast(F32),
+                    in_=turned_of[(m, j)][:].rearrange("p (g u) r -> p g r u", u=2),
+                )
+
+            def quantise_h2(m, i):
+                first, last = CHUNKS[i]
+                if i == 0:
+                    codes = work.tile([P, PASSES * BATCH], U32, name="codes_a_%d" % m, tag="codes_a", align_bytes=64)
+                    plane = work.tile([P, PASSES * BATCH], U8, name="plane_a_%d" % m, tag="plane_a", align_bytes=64)
+                    codes_a_of[m] = (codes, plane)
+                codes, plane = codes_a_of[m]
+                nc.vector.quantize_mx(
+                    out=codes[:, PASSES * first : PASSES * last].bitcast(FP8X4),
+                    scales=plane[:, PASSES * first : PASSES * last],
+                    in_=grouped_a_of[(m, i)][:].rearrange("p g r t -> p (g r t)"),
+                )
+
+            def first_matmul(m, s, h):
+                codes, plane = codes_a_of[m]
+                tile_cols = slice((h * STEPS + s) * P, (h * STEPS + s + 1) * P)
+                wide = psum.tile([P, BANK], F32, name="wide_%d_%d_%d" % (m, s, h), tag="wide")
+                narrow = psum.tile([P, BATCH - BANK], F32, name="narrow_%d_%d_%d" % (m, s, h), tag="narrow")
+                for i in range(len(CHUNKS)):
+                    first, last = CHUNKS[i]
+                    sums = wide[:] if first == 0 else narrow[:, first - BANK : last - BANK]
                     for g in range(PASSES):
-                        start = code_column(q, first, last, g) + j * P - first
+                        c = PASSES * m + g
+                        cols = slice(code_column(i, g), code_column(i, g) + last - first)
                         nc.tensor.matmul_mx(
-                            out=head_of[q][:, j - units_of(q)[0], :],
+                            out=sums,
+                            lhsT=w3_of[m][:, g, tile_cols].bitcast(FP8X4),
+                            lhsT_scale=w3_planes[4 * (c % PLANES_PER_TILE) : P, c // PLANES_PER_TILE, tile_cols],
+                            rhs=codes[:, cols].bitcast(FP8X4),
+                            rhs_scale=plane[:, cols],
+                            start=(g == 0),
+                            stop=(g == PASSES - 1),
+                        )
+                sums_of[(m, s, h)] = (wide, narrow)
+
+            def silu(m, s, h):
+                if h == 0:
+                    rows_of[(m, s)] = work.tile([P, PASSES, BATCH], BF16, name="rows_%d_%d" % (m, s), tag="rows", bufs=4)
+                wide, narrow = sums_of[(m, s, h)]
+                column = (m * PASSES + h) * STEPS + s
+                bias = b3_columns[:, column : column + 1]
+                nc.scalar.activation(out=rows_of[(m, s)][:, h, 0:BANK], in_=wide[:], func=ACT.Silu, bias=bias)
+                nc.scalar.activation(out=rows_of[(m, s)][:, h, BANK:BATCH], in_=narrow[:], func=ACT.Silu, bias=bias)
+
+            def fold(m, s):
+                if s == 0:
+                    folded_of[m] = work.tile([P, PACK, PASSES, BATCH], BF16, name="folded_%d" % m, tag="folded")
+                nc.sync.dma_start(
+                    out=folded_of[m][s:P:STEPS, :, :, :].rearrange("r t g b -> r t (g b)"),
+                    in_=rows_of[(m, s)][:].rearrange("p g b -> p (g b)"),
+                )
+
+            def regroup_h3(m, i):
+                first, last = CHUNKS[i]
+                grouped_c_of[(m, i)] = work.tile(
+                    [P, PASSES, last - first, PACK], BF16, name="grouped_c_%d_%d" % (m, i), tag="grouped_c", align_bytes=64
+                )
+                for g in range(PASSES):
+                    nc.vector.tensor_copy(
+                        out=grouped_c_of[(m, i)][:, g, :, :].rearrange("p (c i) t -> p c t i", i=4),
+                        in_=folded_of[m][:, :, g, first:last].rearrange("p t (c i) -> p c t i", i=4),
+                    )
+
+            def quantise_h3(m, i):
+                first, last = CHUNKS[i]
+                if i == 0:
+                    codes = work.tile([P, PASSES * BATCH], U32, name="codes_c_%d" % m, tag="codes_c", bufs=1, align_bytes=64)
+                    plane = work.tile([P, PASSES * BATCH], U8, name="plane_c_%d" % m, tag="plane_c", bufs=1, align_bytes=64)
+                    codes_c_of[m] = (codes, plane)
+                codes, plane = codes_c_of[m]
+                nc.vector.quantize_mx(
+                    out=codes[:, PASSES * first : PASSES * last].bitcast(FP8X4),
+                    scales=plane[:, PASSES * first : PASSES * last],
+                    in_=grouped_c_of[(m, i)][:].rearrange("p g r t -> p (g r t)"),
+                )
+
+            def second_matmul(m, group):
+                codes, plane = codes_c_of[m]
+                first, last = HEAD_GROUPS[group]
+                head_of[m] = psum.tile([P, BANK // OUT2, OUT2], F32, name="head_%d_%d" % (m, group), tag="head")
+                for j in range(first, last):
+                    i = chunk_of_unit(j)
+                    for g in range(PASSES):
+                        start = code_column(i, g) + j * P - CHUNKS[i][0]
+                        nc.tensor.matmul_mx(
+                            out=head_of[m][:, j - first, :],
                             lhsT=codes[:, start : start + P].bitcast(FP8X4),
                             lhsT_scale=plane[:, start : start + P],
                             rhs=w4_codes[:, PASSES * m + g, :].bitcast(FP8X4),
@@ -278,153 +291,158 @@ def tile_ensembledynamicsmodel_pa_t_e_kernel(
                             stop=(g == PASSES - 1),
                         )
 
-        def add_b4(q):
-            m = q // 2
-            units = units_of(q)
-            if q % 2 == 0:
-                results_of[m] = work.tile([P, 2, UNITS, OUT], F32, name="results_%d" % m, tag="results")
-            nc.vector.tensor_tensor(
-                out=results_of[m][:, :, units[0] : units[0] + len(units), :].rearrange("p h j o -> p j h o"),
-                in0=head_of[q][:, 0 : len(units), :].rearrange("p j (h o) -> p j h o", h=2),
-                in1=shift[:, m, :].rearrange("p (h o) -> p h o", h=2).unsqueeze(1).to_broadcast([P, len(units), 2, OUT]),
-                op=ALU.add,
-            )
+            def add_b4(m, group):
+                first, last = HEAD_GROUPS[group]
+                if group == 0:
+                    results_of[m] = work.tile([P, 2, UNITS, OUT], F32, name="results_%d" % m, tag="results")
+                nc.vector.tensor_tensor(
+                    out=results_of[m][:, :, first:last, :].rearrange("p h j o -> p j h o"),
+                    in0=head_of[m][:, 0 : last - first, :].rearrange("p j (h o) -> p j h o", h=2),
+                    in1=shift[:, m, :].rearrange("p (h o) -> p h o", h=2).unsqueeze(1).to_broadcast([P, last - first, 2, OUT]),
+                    op=ALU.add,
+                )
 
-        def bounds_inputs(m):
-            nc.sync.dma_start(
-                out=out_0[m].rearrange("(p j) o -> p (j o)", j=UNITS),
-                in_=results_of[m][:, 0, :, :].rearrange("p j o -> p (j o)"),
-            )
-            u = results_of[m][:, 1, :, :]
-            minus_size = work.tile(member_shape, F32, name="minus_size_%d" % m, tag="minus_size")
-            nc.vector.scalar_tensor_tensor(out=minus_size[:], in0=u, scalar=-1.0, in1=u, op0=ALU.mult, op1=ALU.min)
-            c = work.tile(member_shape, F32, name="c_%d" % m, tag="c")
-            nc.vector.scalar_tensor_tensor(
-                out=c[:],
-                in0=u,
-                scalar=0.0,
-                in1=span[:].unsqueeze(1).to_broadcast(member_shape),
-                op0=ALU.min,
-                op1=ALU.add,
-            )
-            floor_of[m] = bounds.tile(member_shape, F32, name="floor_%d" % m, tag="floor")
-            nc.vector.scalar_tensor_tensor(
-                out=floor_of[m][:],
-                in0=c[:],
-                scalar=0.0,
-                in1=min_lv[:].unsqueeze(1).to_broadcast(member_shape),
-                op0=ALU.max,
-                op1=ALU.add,
-            )
-            c_of[m] = (minus_size, c)
+            c_of = {}
+            tanh_of = {}
 
-        def bounds_tanh(m):
-            minus_size, c = c_of[m]
-            eta = work.tile(member_shape, F32, name="eta_%d" % m, tag="eta")
-            nc.scalar.activation(out=eta[:], in_=minus_size[:], func=ACT.Tanh, scale=0.5)
-            tau = work.tile(member_shape, F32, name="tau_%d" % m, tag="tau")
-            nc.scalar.activation(out=tau[:], in_=c[:], func=ACT.Tanh, scale=0.5)
-            one_plus_eta = work.tile(member_shape, F32, name="one_plus_eta_%d" % m, tag="one_plus_eta")
-            nc.scalar.activation(out=one_plus_eta[:], in_=eta[:], func=ACT.Identity, bias=one[:])
-            abs_tau_of[m] = bounds.tile(member_shape, F32, name="abs_tau_%d" % m, tag="abs_tau")
-            nc.scalar.activation(out=abs_tau_of[m][:], in_=tau[:], func=ACT.Abs)
-            tanh_of[m] = (one_plus_eta, tau)
+            def bounds_inputs(m):
+                nc.sync.dma_start(
+                    out=out_0[m].rearrange("(p j) o -> p (j o)", j=UNITS),
+                    in_=results_of[m][:, 0, :, :].rearrange("p j o -> p (j o)"),
+                )
+                u = results_of[m][:, 1, :, :]
+                minus_size = work.tile(member_shape, F32, name="minus_size_%d" % m, tag="minus_size")
+                nc.vector.scalar_tensor_tensor(out=minus_size[:], in0=u, scalar=-1.0, in1=u, op0=ALU.mult, op1=ALU.min)
+                c = work.tile(member_shape, F32, name="c_%d" % m, tag="c")
+                nc.vector.scalar_tensor_tensor(
+                    out=c[:],
+                    in0=u,
+                    scalar=0.0,
+                    in1=span[:].unsqueeze(1).to_broadcast(member_shape),
+                    op0=ALU.min,
+                    op1=ALU.add,
+                )
+                floor_of[m] = bounds.tile(member_shape, F32, name="floor_%d" % m, tag="floor")
+                nc.vector.scalar_tensor_tensor(
+                    out=floor_of[m][:],
+                    in0=c[:],
+                    scalar=0.0,
+                    in1=min_lv[:].unsqueeze(1).to_broadcast(member_shape),
+                    op0=ALU.max,
+                    op1=ALU.add,
+                )
+                c_of[m] = (minus_size, c)
 
-        def bounds_product(m):
-            one_plus_eta, tau = tanh_of[m]
-            product_of[m] = bounds.tile(member_shape, F32, name="product_%d" % m, tag="product")
-            nc.vector.scalar_tensor_tensor(
-                out=product_of[m][:], in0=tau[:], scalar=1.0, in1=one_plus_eta[:], op0=ALU.add, op1=ALU.mult
-            )
+            def bounds_tanh(m):
+                minus_size, c = c_of[m]
+                eta = work.tile(member_shape, F32, name="eta_%d" % m, tag="eta")
+                nc.scalar.activation(out=eta[:], in_=minus_size[:], func=ACT.Tanh, scale=0.5)
+                tau = work.tile(member_shape, F32, name="tau_%d" % m, tag="tau")
+                nc.scalar.activation(out=tau[:], in_=c[:], func=ACT.Tanh, scale=0.5)
+                tanh_of[m] = (eta, tau)
 
-        def take_logs(m):
-            nc.scalar.activation(out=product_of[m][:], in_=product_of[m][:], func=ACT.Ln, scale=-0.5, bias=two[:])
-            nc.scalar.activation(out=abs_tau_of[m][:], in_=abs_tau_of[m][:], func=ACT.Ln, bias=one[:])
+            def bounds_product(m):
+                eta, tau = tanh_of[m]
+                one_plus_eta = work.tile(member_shape, F32, name="one_plus_eta_%d" % m, tag="one_plus_eta")
+                nc.vector.tensor_scalar_add(out=one_plus_eta[:], in0=eta[:], scalar1=1.0)
+                product_of[m] = bounds.tile(member_shape, F32, name="product_%d" % m, tag="product")
+                nc.vector.scalar_tensor_tensor(
+                    out=product_of[m][:], in0=tau[:], scalar=1.0, in1=one_plus_eta[:], op0=ALU.add, op1=ALU.mult
+                )
+                abs_tau_of[m] = bounds.tile(member_shape, F32, name="abs_tau_%d" % m, tag="abs_tau")
+                nc.vector.scalar_tensor_tensor(
+                    out=abs_tau_of[m][:], in0=tau[:], scalar=-1.0, in1=tau[:], op0=ALU.mult, op1=ALU.max
+                )
 
-        def finish_bounds(m):
-            nc.vector.tensor_tensor(out=floor_of[m][:], in0=floor_of[m][:], in1=product_of[m][:], op=ALU.add)
-            nc.vector.tensor_tensor(out=floor_of[m][:], in0=floor_of[m][:], in1=abs_tau_of[m][:], op=ALU.subtract)
-            nc.sync.dma_start(
-                out=out_1[m].rearrange("(p j) o -> p (j o)", j=UNITS),
-                in_=floor_of[m][:].rearrange("p j o -> p (j o)"),
-            )
+            def take_logs(m):
+                nc.scalar.activation(out=product_of[m][:], in_=product_of[m][:], func=ACT.Ln, scale=-0.5, bias=two[:])
+                nc.scalar.activation(out=abs_tau_of[m][:], in_=abs_tau_of[m][:], func=ACT.Ln, bias=one[:])
 
-        for q in range(-2, N_HALVES + 2):
-            does_a = 0 <= q + 1 < N_HALVES
-            does_b = 0 <= q < N_HALVES
-            does_c = 0 <= q - 1 < N_HALVES
-            does_d = 0 <= q - 2 < N_HALVES
-            next_member = q // 2 + 1
-            done_member = (q - 2) // 2
-            for s in range(STEPS):
-                units = []
-                if does_a:
-                    units = list(units_of(q + 1))[s * UNITS_PER_STEP : (s + 1) * UNITS_PER_STEP]
-                if s == 0 and 2 <= q + 3 < N_HALVES:
-                    load_h2(q + 3)
-                if s == 2 and q % 2 == 1 and next_member + 1 < MEMBERS:
-                    for h in range(PASSES):
-                        load_w3_half(next_member + 1, h)
+            def finish_bounds(m):
+                nc.vector.tensor_tensor(out=floor_of[m][:], in0=floor_of[m][:], in1=product_of[m][:], op=ALU.add)
+                nc.vector.tensor_tensor(out=floor_of[m][:], in0=floor_of[m][:], in1=abs_tau_of[m][:], op=ALU.subtract)
+                nc.sync.dma_start(
+                    out=out_1[m].rearrange("(p j) o -> p (j o)", j=UNITS),
+                    in_=floor_of[m][:].rearrange("p j o -> p (j o)"),
+                )
 
-                for j in units:
-                    transpose_h2(q + 1, j)
-                if q == -1 and s == STEPS - 1:
-                    nc.vector.tensor_copy(out=b3_rows_f32[:], in_=b3_rows[:])
-                    b3_turned = psum.tile([P, PASSES * 2, P], F32, name="b3_turned", tag="turned")
-                    nc.tensor.transpose(out=b3_turned[:, 0, :], in_=b3_rows_f32[:], identity=ident[:])
-                if does_d and s == 0:
-                    second_matmul(q - 2)
-                if does_b:
-                    for h in range(PASSES):
-                        first_matmul(q, s, h)
+            for e in range(-1, MEMBERS + 1):
+                ahead = e + 1
+                behind = e - 1
+                does_a = ahead < MEMBERS
+                does_b = 0 <= e < MEMBERS
+                does_cd = 0 <= behind
+                for s in range(STEPS):
+                    units = range(s * UNITS_PER_STEP, min((s + 1) * UNITS_PER_STEP, UNITS))
+                    if s == 0 and e + 2 < MEMBERS:
+                        load_h2(e + 2, range(UNITS))
+                    if s == 2 and e + 2 < MEMBERS:
+                        new_w3_raw(e + 2)
+                        for h in range(PASSES):
+                            load_w3_half(e + 2, h)
 
-                if does_a and s == 0:
-                    new_grouped("a", q + 1)
-                for j in units:
-                    copy_out_h2(q + 1, j)
-                if does_b:
-                    for h in range(PASSES):
-                        silu(q, s, h)
-                    fold(q, s)
-                if q % 2 == 1 and s == 1 and 0 <= done_member < MEMBERS - 1:
-                    bounds_tanh(done_member)
+                    if does_a:
+                        for j in units:
+                            transpose_h2(ahead, j)
+                    if e == -1 and s == STEPS - 1:
+                        nc.vector.tensor_copy(out=b3_rows_f32[:], in_=b3_rows[:])
+                        b3_turned = psum.tile([P, PASSES * 2, P], F32, name="b3_turned", tag="turned")
+                        nc.tensor.transpose(out=b3_turned[:, 0, :], in_=b3_rows_f32[:], identity=ident[:])
+                    if does_b:
+                        for h in range(PASSES):
+                            first_matmul(e, s, h)
+                    if does_cd and s >= STEPS - len(HEAD_GROUPS):
+                        second_matmul(behind, s - (STEPS - len(HEAD_GROUPS)))
 
-                if q == -1 and s == STEPS - 1:
-                    nc.vector.tensor_copy(out=b3_columns[:], in_=b3_turned[:, 0, 0 : MEMBERS * PASSES * STEPS])
-                if q == 0 and s == 0:
-                    nc.vector.tensor_copy(out=shift[:, :, 0:OUT], in_=b4_all[:, :, 0:OUT])
-                    nc.vector.tensor_tensor(
-                        out=shift[:, :, OUT:OUT2],
-                        in0=b4_all[:, :, OUT:OUT2],
-                        in1=max_lv[:].unsqueeze(1).to_broadcast([P, MEMBERS, OUT]),
-                        op=ALU.subtract,
-                    )
-                    nc.vector.tensor_tensor(out=span[:], in0=max_lv[:], in1=min_lv[:], op=ALU.subtract)
-                if q % 2 == 0 and s == 0 and 0 <= done_member - 1 < MEMBERS - 1:
-                    bounds_product(done_member - 1)
-                if s == 0 and next_member < MEMBERS:
-                    sort_w3(next_member, q % 2)
-                if does_d and s == 0:
-                    add_b4(q - 2)
-                    if q % 2 == 1 and done_member < MEMBERS - 1:
-                        bounds_inputs(done_member)
-                if does_c and s == 1:
-                    regroup_h3(q - 1)
-                if does_a and s == 2:
-                    quantise("a", q + 1)
-                if does_c and s == 2:
-                    quantise("c", q - 1)
-                if q == N_HALVES and s == 0:
-                    for m in range(MEMBERS - 1):
-                        take_logs(m)
+                    if does_a:
+                        for j in units:
+                            copy_out_h2(ahead, j)
+                    if does_b:
+                        for h in range(PASSES):
+                            silu(e, s, h)
+                        fold(e, s)
 
-        last_member = MEMBERS - 1
-        bounds_inputs(last_member)
-        bounds_tanh(last_member)
-        finish_bounds(0)
-        finish_bounds(1)
-        bounds_product(last_member)
-        take_logs(last_member)
-        finish_bounds(2)
-        finish_bounds(3)
-        finish_bounds(last_member)
+                    if e == -1 and s == STEPS - 1:
+                        nc.vector.tensor_copy(out=b3_columns[:], in_=b3_turned[:, 0, 0 : MEMBERS * PASSES * STEPS])
+                    if e == 0 and s == 0:
+                        nc.vector.tensor_copy(out=shift[:, :, 0:OUT], in_=b4_all[:, :, 0:OUT])
+                        nc.vector.tensor_tensor(
+                            out=shift[:, :, OUT:OUT2],
+                            in0=b4_all[:, :, OUT:OUT2],
+                            in1=max_lv[:].unsqueeze(1).to_broadcast([P, MEMBERS, OUT]),
+                            op=ALU.subtract,
+                        )
+                        nc.vector.tensor_tensor(out=span[:], in0=max_lv[:], in1=min_lv[:], op=ALU.subtract)
+                    if s == 0 and 0 <= e - 2 < MEMBERS - 1:
+                        bounds_product(e - 2)
+                    if does_a and s == 0:
+                        sort_w3(ahead, 0)
+                    if does_cd and s < len(CHUNKS):
+                        regroup_h3(behind, s)
+                    if does_a:
+                        for i in range(len(CHUNKS)):
+                            if (CHUNKS[i][1] // P - 1) // UNITS_PER_STEP == s:
+                                quantise_h2(ahead, i)
+                    if does_a and s == 1:
+                        sort_w3(ahead, 1)
+                    if does_cd and s < len(CHUNKS):
+                        quantise_h3(behind, s)
+                    if does_cd and s >= STEPS - len(HEAD_GROUPS):
+                        add_b4(behind, s - (STEPS - len(HEAD_GROUPS)))
+                    if e == MEMBERS and s == 0:
+                        for m in range(MEMBERS - 1):
+                            take_logs(m)
+                    if does_cd and s == STEPS - 1 and behind < MEMBERS - 1:
+                        bounds_inputs(behind)
+                        bounds_tanh(behind)
+
+            last_member = MEMBERS - 1
+            bounds_inputs(last_member)
+            bounds_tanh(last_member)
+            finish_bounds(0)
+            finish_bounds(1)
+            bounds_product(last_member)
+            take_logs(last_member)
+            finish_bounds(2)
+            finish_bounds(3)
+            finish_bounds(last_member)

from contextlib import ExitStack

import concourse.mybir as mybir
from concourse.masks import make_identity

F32 = mybir.dt.float32
BF16 = mybir.dt.bfloat16
I32 = mybir.dt.int32
U32 = mybir.dt.uint32
U8 = mybir.dt.uint8
FP8X4 = mybir.dt.float8_e4m3fn_x4
ACT = mybir.ActivationFunctionType
ALU = mybir.AluOpType

MEMBERS = 5
BATCH = 896
HIDDEN = 1024
OUT = 64
OUT2 = 2 * OUT

P = 128
PACK = 4
K_PASS = P * PACK
PASSES = HIDDEN // K_PASS
BANK = 512
UNITS = BATCH // P
CHUNKS = ((0, 512), (512, 768), (768, 896))
PLANES_PER_TILE = 4
HEAD_GROUPS = ((0, 4), (4, 7))
STEPS = 4
UNITS_PER_STEP = 2

FLOPS = 2 * MEMBERS * BATCH * HIDDEN * (HIDDEN + OUT2)


def tile_ensembledynamicsmodel_pa_t_e_kernel(
    tc, h2, w3_words, w3_scales, b3, w4_words, w4_scales, b4, max_logvar, min_logvar, out_0, out_1
):
    nc = tc.nc
    member_shape = [P, UNITS, OUT]
    with ExitStack() as whole:
        keep = whole.enter_context(tc.tile_pool(name="keep", bufs=1))
        bounds = whole.enter_context(tc.tile_pool(name="bounds", bufs=MEMBERS))
        whole.enter_context(tc.manual_schedule())

        ident = keep.tile([P, P], F32)
        make_identity(nc, ident[:])
        one = keep.tile([P, 1], F32)
        nc.vector.memset(one[:], 1.0)
        two = keep.tile([P, 1], F32)
        nc.vector.memset(two[:], 2.0)
        warm = keep.tile([P, 1], F32)
        nc.scalar.activation(out=warm[:], in_=one[:], func=ACT.Silu)

        n_passes = MEMBERS * PASSES
        n_plane_tiles = (n_passes + PLANES_PER_TILE - 1) // PLANES_PER_TILE
        w3_planes_raw = keep.tile([P, n_plane_tiles, HIDDEN], U8)
        nc.vector.memset(w3_planes_raw[:].rearrange("p a n -> p (a n)").bitcast(I32), 0)
        w3_planes = keep.tile([P, n_plane_tiles, HIDDEN], U8, align_bytes=64)
        w4_planes = keep.tile([P, n_passes, OUT2], U8, align_bytes=64)
        nc.vector.memset(w4_planes[:].rearrange("p c n -> p (c n)").bitcast(I32), 0)
        w4_codes = keep.tile([P, n_passes, OUT2], U32, align_bytes=64)

        b3_rows = keep.tile([P, P], BF16)
        nc.vector.memset(b3_rows[:], 0.0)
        b3_rows_f32 = keep.tile([P, P], F32)
        b3_columns = keep.tile([P, MEMBERS * PASSES * STEPS], F32)
        b4_all = keep.tile([P, MEMBERS, OUT2], BF16)
        max_lv = keep.tile([P, OUT], BF16)
        min_lv = keep.tile([P, OUT], BF16)
        shift = keep.tile([P, MEMBERS, OUT2], F32)
        span = keep.tile([P, OUT], F32)

        product_of = {}
        abs_tau_of = {}
        floor_of = {}

        with ExitStack() as main:
            loads = main.enter_context(tc.tile_pool(name="loads", bufs=2))
            work = main.enter_context(tc.tile_pool(name="work", bufs=2))
            psum = main.enter_context(tc.psum_pool(name="psum", bufs=2))

            h2_of = {}
            w3_raw_of = {}
            w3_of = {}
            grouped_a_of = {}
            turned_of = {}
            codes_a_of = {}
            sums_of = {}
            rows_of = {}
            folded_of = {}
            grouped_c_of = {}
            codes_c_of = {}
            head_of = {}
            results_of = {}

            def load_h2(m, units):
                if units[0] == 0:
                    h2_of[m] = loads.tile([P, UNITS, HIDDEN], BF16, name="h2_%d" % m, tag="h2")
                rows = h2[m].rearrange("(p j) k -> p j k", j=UNITS)
                first, last = units[0], units[0] + len(units)
                nc.sync.dma_start(out=h2_of[m][:, first:last, :], in_=rows[:, first:last, :])

            def load_w3_half(m, h):
                words = w3_words[PASSES * m : PASSES * (m + 1)].rearrange("g p n t -> p g (n t)")
                nc.sync.dma_start(
                    out=w3_raw_of[m][:, :, h * K_PASS : (h + 1) * K_PASS].bitcast(I32),
                    in_=words[:, :, h * K_PASS * PACK : (h + 1) * K_PASS * PACK].bitcast(I32),
                )

            def load_w3_planes(a):
                first = a * PLANES_PER_TILE
                n_planes = min(PLANES_PER_TILE, n_passes - first)
                for quadrant in range(4):
                    nc.sync.dma_start(
                        out=w3_planes_raw[32 * quadrant : 32 * quadrant + 4 * n_planes, a, :].bitcast(I32),
                        in_=w3_scales[first : first + n_planes, 4 * quadrant : 4 * quadrant + 4, :].bitcast(I32),
                    )

            def new_w3_raw(m):
                w3_raw_of[m] = loads.tile([P, PASSES, HIDDEN], U32, name="w3_raw_%d" % m, tag="w3_raw", bufs=1)

            new_w3_raw(0)
            load_w3_half(0, 0)
            load_w3_planes(0)
            load_h2(0, range(0, CHUNKS[0][1] // P))
            load_w3_half(0, 1)
            load_h2(0, range(CHUNKS[0][1] // P, UNITS))
            b3_view = b3.rearrange("e o (h r s t) -> s (e o h) r t", h=PASSES, s=STEPS, t=PACK)
            for s in range(STEPS):
                nc.sync.dma_start(
                    out=b3_rows[s : MEMBERS * PASSES * STEPS : STEPS, :].rearrange("c (r t) -> c r t", t=PACK),
                    in_=b3_view[s],
                )
            for a in range(1, n_plane_tiles):
                load_w3_planes(a)
            for quadrant in range(4):
                nc.sync.dma_start(
                    out=w4_planes[32 * quadrant : 32 * quadrant + 4, :, :].bitcast(I32),
                    in_=w4_scales[:, 4 * quadrant : 4 * quadrant + 4, :].rearrange("c r n -> r c n").bitcast(I32),
                )
            nc.sync.dma_start(
                out=w4_codes[:].bitcast(I32),
                in_=w4_words.rearrange("c p n t -> p c (n t)").bitcast(I32),
            )
            nc.sync.dma_start(
                out=b4_all[:].rearrange("p e n -> p (e n)"),
                in_=b4.rearrange("e o n -> (e o n)").partition_broadcast(P),
            )
            nc.sync.dma_start(out=max_lv[:], in_=max_logvar[0, :].partition_broadcast(P))
            nc.sync.dma_start(out=min_lv[:], in_=min_logvar[0, :].partition_broadcast(P))

            def sort_w3(m, h):
                if h == 0:
                    w3_of[m] = work.tile([P, PASSES, HIDDEN], U32, name="w3_%d" % m, tag="w3", align_bytes=64)
                cols = slice(h * K_PASS, (h + 1) * K_PASS)
                if (PASSES * m) % PLANES_PER_TILE == 0:
                    a = (PASSES * m) // PLANES_PER_TILE
                    nc.vector.tensor_copy(
                        out=w3_planes[:, a, cols].bitcast(I32).rearrange("p (s r) -> p s r", s=STEPS),
                        in_=w3_planes_raw[:, a, cols].bitcast(I32).rearrange("p (r s) -> p s r", s=STEPS),
                    )
                for g in range(PASSES):
                    nc.vector.tensor_copy(
                        out=w3_of[m][:, g, cols].bitcast(I32).rearrange("p (s r t) -> p s r t", s=STEPS, t=PACK),
                        in_=w3_raw_of[m][:, g, cols].bitcast(I32).rearrange("p (r s t) -> p s r t", s=STEPS, t=PACK),
                    )

            def chunk_of_unit(j):
                return [i for i in range(len(CHUNKS)) if CHUNKS[i][0] <= j * P < CHUNKS[i][1]][0]

            def code_column(i, g):
                first, last = CHUNKS[i]
                return PASSES * first + g * (last - first)

            def transpose_h2(m, j):
                words = h2_of[m][:, j, :].bitcast(F32)
                bank = psum.tile([P, PASSES * 2, P], F32, name="turned_%d_%d" % (m, j), tag="turned")
                for g in range(PASSES):
                    for u in range(2):
                        nc.tensor.transpose(
                            out=bank[:, 2 * g + u, :],
                            in_=words[:, 256 * g + u : 256 * (g + 1) : 2],
                            identity=ident[:],
                        )
                turned_of[(m, j)] = bank

            def copy_out_h2(m, j):
                i = chunk_of_unit(j)
                first, last = CHUNKS[i]
                if j * P == first:
                    grouped_a_of[(m, i)] = work.tile(
                        [P, PASSES, last - first, PACK], BF16, name="grouped_a_%d_%d" % (m, i), tag="grouped_a", align_bytes=64
                    )
                nc.scalar.copy(
                    out=grouped_a_of[(m, i)][:, :, j * P - first : (j + 1) * P - first, :].bitcast(F32),
                    in_=turned_of[(m, j)][:].rearrange("p (g u) r -> p g r u", u=2),
                )

            def quantise_h2(m, i):
                first, last = CHUNKS[i]
                if i == 0:
                    codes = work.tile([P, PASSES * BATCH], U32, name="codes_a_%d" % m, tag="codes_a", align_bytes=64)
                    plane = work.tile([P, PASSES * BATCH], U8, name="plane_a_%d" % m, tag="plane_a", align_bytes=64)
                    codes_a_of[m] = (codes, plane)
                codes, plane = codes_a_of[m]
                nc.vector.quantize_mx(
                    out=codes[:, PASSES * first : PASSES * last].bitcast(FP8X4),
                    scales=plane[:, PASSES * first : PASSES * last],
                    in_=grouped_a_of[(m, i)][:].rearrange("p g r t -> p (g r t)"),
                )

            def first_matmul(m, s, h):
                codes, plane = codes_a_of[m]
                tile_cols = slice((h * STEPS + s) * P, (h * STEPS + s + 1) * P)
                wide = psum.tile([P, BANK], F32, name="wide_%d_%d_%d" % (m, s, h), tag="wide")
                narrow = psum.tile([P, BATCH - BANK], F32, name="narrow_%d_%d_%d" % (m, s, h), tag="narrow")
                for i in range(len(CHUNKS)):
                    first, last = CHUNKS[i]
                    sums = wide[:] if first == 0 else narrow[:, first - BANK : last - BANK]
                    for g in range(PASSES):
                        c = PASSES * m + g
                        cols = slice(code_column(i, g), code_column(i, g) + last - first)
                        nc.tensor.matmul_mx(
                            out=sums,
                            lhsT=w3_of[m][:, g, tile_cols].bitcast(FP8X4),
                            lhsT_scale=w3_planes[4 * (c % PLANES_PER_TILE) : P, c // PLANES_PER_TILE, tile_cols],
                            rhs=codes[:, cols].bitcast(FP8X4),
                            rhs_scale=plane[:, cols],
                            start=(g == 0),
                            stop=(g == PASSES - 1),
                        )
                sums_of[(m, s, h)] = (wide, narrow)

            def silu(m, s, h):
                if h == 0:
                    rows_of[(m, s)] = work.tile([P, PASSES, BATCH], BF16, name="rows_%d_%d" % (m, s), tag="rows", bufs=4)
                wide, narrow = sums_of[(m, s, h)]
                column = (m * PASSES + h) * STEPS + s
                bias = b3_columns[:, column : column + 1]
                nc.scalar.activation(out=rows_of[(m, s)][:, h, 0:BANK], in_=wide[:], func=ACT.Silu, bias=bias)
                nc.scalar.activation(out=rows_of[(m, s)][:, h, BANK:BATCH], in_=narrow[:], func=ACT.Silu, bias=bias)

            def fold(m, s):
                if s == 0:
                    folded_of[m] = work.tile([P, PACK, PASSES, BATCH], BF16, name="folded_%d" % m, tag="folded")
                nc.sync.dma_start(
                    out=folded_of[m][s:P:STEPS, :, :, :].rearrange("r t g b -> r t (g b)"),
                    in_=rows_of[(m, s)][:].rearrange("p g b -> p (g b)"),
                )

            def regroup_h3(m, i):
                first, last = CHUNKS[i]
                grouped_c_of[(m, i)] = work.tile(
                    [P, PASSES, last - first, PACK], BF16, name="grouped_c_%d_%d" % (m, i), tag="grouped_c", align_bytes=64
                )
                for g in range(PASSES):
                    nc.vector.tensor_copy(
                        out=grouped_c_of[(m, i)][:, g, :, :].rearrange("p (c i) t -> p c t i", i=4),
                        in_=folded_of[m][:, :, g, first:last].rearrange("p t (c i) -> p c t i", i=4),
                    )

            def quantise_h3(m, i):
                first, last = CHUNKS[i]
                if i == 0:
                    codes = work.tile([P, PASSES * BATCH], U32, name="codes_c_%d" % m, tag="codes_c", bufs=1, align_bytes=64)
                    plane = work.tile([P, PASSES * BATCH], U8, name="plane_c_%d" % m, tag="plane_c", bufs=1, align_bytes=64)
                    codes_c_of[m] = (codes, plane)
                codes, plane = codes_c_of[m]
                nc.vector.quantize_mx(
                    out=codes[:, PASSES * first : PASSES * last].bitcast(FP8X4),
                    scales=plane[:, PASSES * first : PASSES * last],
                    in_=grouped_c_of[(m, i)][:].rearrange("p g r t -> p (g r t)"),
                )

            def second_matmul(m, group):
                codes, plane = codes_c_of[m]
                first, last = HEAD_GROUPS[group]
                head_of[m] = psum.tile([P, BANK // OUT2, OUT2], F32, name="head_%d_%d" % (m, group), tag="head")
                for j in range(first, last):
                    i = chunk_of_unit(j)
                    for g in range(PASSES):
                        start = code_column(i, g) + j * P - CHUNKS[i][0]
                        nc.tensor.matmul_mx(
                            out=head_of[m][:, j - first, :],
                            lhsT=codes[:, start : start + P].bitcast(FP8X4),
                            lhsT_scale=plane[:, start : start + P],
                            rhs=w4_codes[:, PASSES * m + g, :].bitcast(FP8X4),
                            rhs_scale=w4_planes[:, PASSES * m + g, :],
                            start=(g == 0),
                            stop=(g == PASSES - 1),
                        )

            def add_b4(m, group):
                first, last = HEAD_GROUPS[group]
                if group == 0:
                    results_of[m] = work.tile([P, 2, UNITS, OUT], F32, name="results_%d" % m, tag="results")
                nc.vector.tensor_tensor(
                    out=results_of[m][:, :, first:last, :].rearrange("p h j o -> p j h o"),
                    in0=head_of[m][:, 0 : last - first, :].rearrange("p j (h o) -> p j h o", h=2),
                    in1=shift[:, m, :].rearrange("p (h o) -> p h o", h=2).unsqueeze(1).to_broadcast([P, last - first, 2, OUT]),
                    op=ALU.add,
                )

            c_of = {}
            tanh_of = {}

            def bounds_inputs(m):
                nc.sync.dma_start(
                    out=out_0[m].rearrange("(p j) o -> p (j o)", j=UNITS),
                    in_=results_of[m][:, 0, :, :].rearrange("p j o -> p (j o)"),
                )
                u = results_of[m][:, 1, :, :]
                minus_size = work.tile(member_shape, F32, name="minus_size_%d" % m, tag="minus_size")
                nc.vector.scalar_tensor_tensor(out=minus_size[:], in0=u, scalar=-1.0, in1=u, op0=ALU.mult, op1=ALU.min)
                c = work.tile(member_shape, F32, name="c_%d" % m, tag="c")
                nc.vector.scalar_tensor_tensor(
                    out=c[:],
                    in0=u,
                    scalar=0.0,
                    in1=span[:].unsqueeze(1).to_broadcast(member_shape),
                    op0=ALU.min,
                    op1=ALU.add,
                )
                floor_of[m] = bounds.tile(member_shape, F32, name="floor_%d" % m, tag="floor")
                nc.vector.scalar_tensor_tensor(
                    out=floor_of[m][:],
                    in0=c[:],
                    scalar=0.0,
                    in1=min_lv[:].unsqueeze(1).to_broadcast(member_shape),
                    op0=ALU.max,
                    op1=ALU.add,
                )
                c_of[m] = (minus_size, c)

            def bounds_tanh(m):
                minus_size, c = c_of[m]
                eta = work.tile(member_shape, F32, name="eta_%d" % m, tag="eta")
                nc.scalar.activation(out=eta[:], in_=minus_size[:], func=ACT.Tanh, scale=0.5)
                tau = work.tile(member_shape, F32, name="tau_%d" % m, tag="tau")
                nc.scalar.activation(out=tau[:], in_=c[:], func=ACT.Tanh, scale=0.5)
                tanh_of[m] = (eta, tau)

            def bounds_product(m):
                eta, tau = tanh_of[m]
                one_plus_eta = work.tile(member_shape, F32, name="one_plus_eta_%d" % m, tag="one_plus_eta")
                nc.vector.tensor_scalar_add(out=one_plus_eta[:], in0=eta[:], scalar1=1.0)
                product_of[m] = bounds.tile(member_shape, F32, name="product_%d" % m, tag="product")
                nc.vector.scalar_tensor_tensor(
                    out=product_of[m][:], in0=tau[:], scalar=1.0, in1=one_plus_eta[:], op0=ALU.add, op1=ALU.mult
                )
                abs_tau_of[m] = bounds.tile(member_shape, F32, name="abs_tau_%d" % m, tag="abs_tau")
                nc.vector.scalar_tensor_tensor(
                    out=abs_tau_of[m][:], in0=tau[:], scalar=-1.0, in1=tau[:], op0=ALU.mult, op1=ALU.max
                )

            def take_logs(m):
                nc.scalar.activation(out=product_of[m][:], in_=product_of[m][:], func=ACT.Ln, scale=-0.5, bias=two[:])
                nc.scalar.activation(out=abs_tau_of[m][:], in_=abs_tau_of[m][:], func=ACT.Ln, bias=one[:])

            def finish_bounds(m):
                nc.vector.tensor_tensor(out=floor_of[m][:], in0=floor_of[m][:], in1=product_of[m][:], op=ALU.add)
                nc.vector.tensor_tensor(out=floor_of[m][:], in0=floor_of[m][:], in1=abs_tau_of[m][:], op=ALU.subtract)
                nc.sync.dma_start(
                    out=out_1[m].rearrange("(p j) o -> p (j o)", j=UNITS),
                    in_=floor_of[m][:].rearrange("p j o -> p (j o)"),
                )

            for e in range(-1, MEMBERS + 1):
                ahead = e + 1
                behind = e - 1
                does_a = ahead < MEMBERS
                does_b = 0 <= e < MEMBERS
                does_cd = 0 <= behind
                for s in range(STEPS):
                    units = range(s * UNITS_PER_STEP, min((s + 1) * UNITS_PER_STEP, UNITS))
                    if s == 0 and e + 2 < MEMBERS:
                        load_h2(e + 2, range(UNITS))
                    if s == 2 and e + 2 < MEMBERS:
                        new_w3_raw(e + 2)
                        for h in range(PASSES):
                            load_w3_half(e + 2, h)

                    if does_a:
                        for j in units:
                            transpose_h2(ahead, j)
                    if e == -1 and s == STEPS - 1:
                        nc.vector.tensor_copy(out=b3_rows_f32[:], in_=b3_rows[:])
                        b3_turned = psum.tile([P, PASSES * 2, P], F32, name="b3_turned", tag="turned")
                        nc.tensor.transpose(out=b3_turned[:, 0, :], in_=b3_rows_f32[:], identity=ident[:])
                    if does_b:
                        for h in range(PASSES):
                            first_matmul(e, s, h)
                    if does_cd and s >= STEPS - len(HEAD_GROUPS):
                        second_matmul(behind, s - (STEPS - len(HEAD_GROUPS)))

                    if does_a:
                        for j in units:
                            copy_out_h2(ahead, j)
                    if does_b:
                        for h in range(PASSES):
                            silu(e, s, h)
                        fold(e, s)

                    if e == -1 and s == STEPS - 1:
                        nc.vector.tensor_copy(out=b3_columns[:], in_=b3_turned[:, 0, 0 : MEMBERS * PASSES * STEPS])
                    if e == 0 and s == 0:
                        nc.vector.tensor_copy(out=shift[:, :, 0:OUT], in_=b4_all[:, :, 0:OUT])
                        nc.vector.tensor_tensor(
                            out=shift[:, :, OUT:OUT2],
                            in0=b4_all[:, :, OUT:OUT2],
                            in1=max_lv[:].unsqueeze(1).to_broadcast([P, MEMBERS, OUT]),
                            op=ALU.subtract,
                        )
                        nc.vector.tensor_tensor(out=span[:], in0=max_lv[:], in1=min_lv[:], op=ALU.subtract)
                    if s == 0 and 0 <= e - 2 < MEMBERS - 1:
                        bounds_product(e - 2)
                    if does_a and s == 0:
                        sort_w3(ahead, 0)
                    if does_cd and s < len(CHUNKS):
                        regroup_h3(behind, s)
                    if does_a:
                        for i in range(len(CHUNKS)):
                            if (CHUNKS[i][1] // P - 1) // UNITS_PER_STEP == s:
                                quantise_h2(ahead, i)
                    if does_a and s == 1:
                        sort_w3(ahead, 1)
                    if does_cd and s < len(CHUNKS):
                        quantise_h3(behind, s)
                    if does_cd and s >= STEPS - len(HEAD_GROUPS):
                        add_b4(behind, s - (STEPS - len(HEAD_GROUPS)))
                    if e == MEMBERS and s == 0:
                        for m in range(MEMBERS - 1):
                            take_logs(m)
                    if does_cd and s == STEPS - 1 and behind < MEMBERS - 1:
                        bounds_inputs(behind)
                        bounds_tanh(behind)

            last_member = MEMBERS - 1
            bounds_inputs(last_member)
            bounds_tanh(last_member)
            finish_bounds(0)
            finish_bounds(1)
            bounds_product(last_member)
            take_logs(last_member)
            finish_bounds(2)
            finish_bounds(3)
            finish_bounds(last_member)
